import numpy as np
import ml_dtypes


def mxq(x, axis, fmt="e4m3"):
    dtype, down = {"e4m3": (ml_dtypes.float8_e4m3fn, 7), "e5m2": (ml_dtypes.float8_e5m2, 14)}[fmt]
    v = np.moveaxis(np.asarray(x, np.float32).astype(ml_dtypes.bfloat16).astype(np.float64), axis, -1)
    blocks = v.reshape(v.shape[:-1] + (-1, 32))
    amax = np.abs(blocks).max(-1, keepdims=True)
    byte = np.maximum(np.where(amax > 0, np.frexp(amax)[1] - 1 + 127, 0) - down, 1)
    scale = np.exp2(byte - 127.0)
    codes = (blocks / scale).astype(np.float32).astype(dtype).astype(np.float64)
    return np.moveaxis((codes * scale).reshape(v.shape), -1, axis)


WIDE = False


def mx_kscale(k):
    if not WIDE:
        return np.ones(k)
    levels = np.array([10, -10, 5, -5, 0])
    a = np.random.permutation(np.resize(levels, k // 512 * 4)).reshape(k // 512, 4)
    idx = np.arange(k)
    return np.exp2(a[idx // 512, idx % 128 // 32])


BF16 = ml_dtypes.bfloat16


def bf(x):
    return np.asarray(x, np.float32).astype(BF16)


def f64(x):
    return np.asarray(x).astype(np.float64)


E2M1 = np.array([0.0, 0.5, 1.0, 1.5, 2.0, 3.0, 4.0, 6.0, -0.0, -0.5, -1.0, -1.5, -2.0, -3.0, -4.0, -6.0])


def pack_weight(w, fmt):
    k, n = w.shape
    w = f64(bf(w)).reshape(k // 32, 32, n)
    amax = np.abs(w).max(1)
    if fmt == "e4m3":
        byte = np.frexp(amax)[1] - 1 + 127 - 7
    else:
        mant, ex = np.frexp(amax / 6.0)
        byte = np.where(mant > 0.5, ex, ex - 1) + 127
    byte = np.clip(np.where(amax > 0, byte, 1), 1, 254)
    scaled = (w * np.exp2(127.0 - byte)[:, None, :]).reshape(k, n).astype(np.float32)
    by_word = np.ascontiguousarray(scaled.reshape(k // 512, 128, 4, n).transpose(0, 1, 3, 2))
    if fmt == "e4m3":
        words = by_word.astype(ml_dtypes.float8_e4m3fn).view(np.uint8)
    else:
        c = by_word.astype(ml_dtypes.float4_e2m1fn).view(np.uint8) & 0xF
        words = c[..., 0::2] | (c[..., 1::2] << 4)
    return np.ascontiguousarray(words), np.ascontiguousarray(byte.astype(np.uint8).reshape(k // 512, 16, n))


def unpack_weight(words, scales, fmt):
    g, p, n, _ = words.shape
    if fmt == "e4m3":
        vals = np.ascontiguousarray(words).view(ml_dtypes.float8_e4m3fn).astype(np.float64)
    else:
        nib = np.empty((g, p, n, 4), np.uint8)
        nib[..., 0::2] = words & 0xF
        nib[..., 1::2] = words >> 4
        vals = E2M1[nib]
    vals = vals * np.repeat(np.exp2(scales.astype(np.float64) - 127.0), 8, axis=1)[..., None]
    return vals.transpose(0, 1, 3, 2).reshape(g * 512, n)


B, T, D, H, HK, HD, W = 4, 2048, 1024, 2, 1, 128, 512
HALF = HD // 2
ROPE_BASE = 10000.0
EPS = 1e-6
FMT = "e4m3"


def rope_cos_sin():
    inv_freq = 1.0 / ROPE_BASE ** (np.arange(0, HD, 2) / HD)
    freqs = np.arange(T)[:, None] * inv_freq[None, :]
    emb = np.concatenate([freqs, freqs], axis=-1)
    return np.cos(emb), np.sin(emb)


def rotate_half(u):
    return np.concatenate([-u[..., HALF:], u[..., :HALF]], axis=-1)


def heads(u, n):
    return u.reshape(B, T, n, HD).transpose(0, 2, 1, 3)


def l2_gain(u, gamma):
    return u / (np.sqrt((u * u).sum(-1, keepdims=True)) + EPS) * gamma


def setup_inputs():
    s = mx_kscale(D)
    x = bf(np.random.standard_normal((B, T, D)) * s)
    wq = np.random.standard_normal((H * HD, D)) / np.sqrt(D) / s[None, :]
    wk = np.random.standard_normal((HK * HD, D)) / np.sqrt(D) / s[None, :]
    wv = np.random.standard_normal((HK * HD, D)) * 2.0 / np.sqrt(D) / s[None, :]
    gamma_q = bf(np.sqrt(HD) * (1.0 + 0.1 * np.random.standard_normal(HD)))
    gamma_k = bf(np.sqrt(HD) * (1.0 + 0.1 * np.random.standard_normal(HD)))
    wq_words, wq_scales = pack_weight(np.ascontiguousarray(wq.T), FMT)
    wk_words, wk_scales = pack_weight(np.ascontiguousarray(wk.T), FMT)
    wv_words, wv_scales = pack_weight(np.ascontiguousarray(wv.T), FMT)
    return {"x": x,
            "wq_words": wq_words, "wq_scales": wq_scales,
            "wk_words": wk_words, "wk_scales": wk_scales,
            "wv_words": wv_words, "wv_scales": wv_scales,
            "gamma_q": gamma_q,
            "gamma_k": gamma_k}


def reference(x, wq_words, wq_scales, wk_words, wk_scales, wv_words, wv_scales, gamma_q, gamma_k):
    xq = mxq(f64(x), 2, "e4m3")
    q = heads(xq @ unpack_weight(wq_words, wq_scales, FMT), H)
    k = heads(xq @ unpack_weight(wk_words, wk_scales, FMT), HK)
    v = heads(xq @ unpack_weight(wv_words, wv_scales, FMT), HK)
    cos, sin = rope_cos_sin()
    q = q * cos + rotate_half(q) * sin
    k = k * cos + rotate_half(k) * sin
    q = l2_gain(q, f64(gamma_q))
    k = l2_gain(k, f64(gamma_k))
    return q, k, v

@@ -1,0 +1,332 @@
+import math
+from contextlib import ExitStack
+
+import concourse.mybir as mybir
+from concourse.masks import make_identity
+
+F32 = mybir.dt.float32
+BF16 = mybir.dt.bfloat16
+I32 = mybir.dt.int32
+U32 = mybir.dt.uint32
+U8 = mybir.dt.uint8
+FP8X4 = mybir.dt.float8_e4m3fn_x4
+ALU = mybir.AluOpType
+ACT = mybir.ActivationFunctionType
+
+P = 128
+B, T, D = 4, 2048, 1024
+HD = 128
+HALF = HD // 2
+Q_HEADS = 2
+ROPED = Q_HEADS + 1
+N_ALL = (ROPED + 1) * HD
+K_PASS = 4 * P
+PASSES = D // K_PASS
+ROPE_BASE = 10000.0
+EPS = 1e-6
+
+J = T // P
+CHUNK = 4
+PAIR = 2
+CHUNKS = B * J // CHUNK
+PAIRS = CHUNKS * CHUNK // PAIR
+X_BUFS = 4
+ROUND_MAGIC = 1.5 * 2.0**23
+
+FLOPS = 2 * B * T * D * N_ALL
+
+
+def tile_gqaattention_pa_t_kernel(
+    tc,
+    x,
+    wq_words,
+    wq_scales,
+    wk_words,
+    wk_scales,
+    wv_words,
+    wv_scales,
+    gamma_q,
+    gamma_k,
+    out_0,
+    out_1,
+    out_2,
+):
+    nc = tc.nc
+    with ExitStack() as ctx:
+        ctx.enter_context(tc.manual_schedule())
+        const = ctx.enter_context(tc.tile_pool(name="const", bufs=1))
+        x_pool = ctx.enter_context(tc.tile_pool(name="x", bufs=X_BUFS))
+        quant = ctx.enter_context(tc.tile_pool(name="quant", bufs=3))
+        norm = ctx.enter_context(tc.tile_pool(name="norm", bufs=3))
+        terms = ctx.enter_context(tc.tile_pool(name="terms", bufs=3))
+        results = ctx.enter_context(tc.tile_pool(name="results", bufs=3))
+        psum_xt = ctx.enter_context(tc.psum_pool(name="psum_xt", bufs=2 * PAIR))
+        psum_acc = ctx.enter_context(tc.psum_pool(name="psum_acc", bufs=2 * PAIR))
+
+        x_view = x.rearrange("b (p j) k -> b p j k", j=J)
+        q_view = out_0.rearrange("b h (p j) d -> b p h j d", j=J)
+        k_view = out_1.rearrange("b h (p j) d -> b p h j d", j=J)
+        v_view = out_2.rearrange("b h (p j) d -> b p h j d", j=J)
+
+        x_tiles = {}
+
+        def load_chunk(c):
+            j0, b = CHUNK * (c // B), c % B
+            x_sb = x_pool.tile([P, CHUNK, D], BF16, name="x_sb")
+            nc.sync.dma_start(out=x_sb[:], in_=x_view[b, :, j0 : j0 + CHUNK, :])
+            x_tiles[c] = x_sb
+
+        load_chunk(0)
+        gamma_bf = const.tile([P, 2, HD], BF16)
+        nc.sync.dma_start(out=gamma_bf[:, 0, :], in_=gamma_q.partition_broadcast(P))
+        nc.sync.dma_start(out=gamma_bf[:, 1, :], in_=gamma_k.partition_broadcast(P))
+
+        w_words = const.tile([P, PASSES, N_ALL], U32, align_bytes=64)
+        w_scales = const.tile([P, PASSES, N_ALL], U8, align_bytes=64)
+        nc.vector.memset(w_scales[:].bitcast(I32), 0)
+        first = 0
+        for words, scales in ((wq_words, wq_scales), (wk_words, wk_scales), (wv_words, wv_scales)):
+            cols = slice(first, first + words.shape[2])
+            first += words.shape[2]
+            for quadrant in range(4):
+                nc.sync.dma_start(
+                    out=w_scales[32 * quadrant : 32 * quadrant + 4, :, cols].bitcast(I32),
+                    in_=scales[:, 4 * quadrant : 4 * quadrant + 4, :]
+                    .rearrange("g r n -> r g n")
+                    .bitcast(I32),
+                )
+            nc.sync.dma_start(
+                out=w_words[:, :, cols].bitcast(I32),
+                in_=words.rearrange("g p n t -> p g (n t)").bitcast(I32),
+            )
+
+        for c in range(1, X_BUFS):
+            load_chunk(c)
+
+        position_i = const.tile([P, J], I32)
+        nc.gpsimd.iota(position_i[:], pattern=[[1, J]], base=0, channel_multiplier=J)
+        ident = const.tile([P, P], F32)
+        make_identity(nc, ident[:])
+
+        one = const.tile([P, 1], F32)
+        nc.vector.memset(one[:], 1.0)
+        quarter_turn = const.tile([P, 1], F32)
+        nc.vector.tensor_scalar_mul(out=quarter_turn[:], in0=one[:], scalar1=math.pi / 2)
+        freq = const.tile([P, HALF], F32)
+        nc.vector.tensor_scalar_mul(out=freq[:, 0:1], in0=one[:], scalar1=1.0 / (2.0 * math.pi))
+        width = 1
+        while width < HALF:
+            nc.vector.tensor_scalar_mul(
+                out=freq[:, width : 2 * width],
+                in0=freq[:, 0:width],
+                scalar1=ROPE_BASE ** (-width / HALF),
+            )
+            width *= 2
+        position = const.tile([P, J], F32)
+        nc.vector.tensor_copy(out=position[:], in_=position_i[:])
+        turns = const.tile([P, J, HALF], F32)
+        nc.vector.tensor_tensor(
+            out=turns[:],
+            in0=position[:].unsqueeze(2).to_broadcast([P, J, HALF]),
+            in1=freq[:].unsqueeze(1).to_broadcast([P, J, HALF]),
+            op=ALU.mult,
+        )
+        whole = const.tile([P, J, HALF], F32)
+        nc.vector.tensor_scalar(
+            out=whole[:],
+            in0=turns[:],
+            scalar1=ROUND_MAGIC,
+            scalar2=ROUND_MAGIC,
+            op0=ALU.add,
+            op1=ALU.subtract,
+        )
+        frac = const.tile([P, J, HALF], F32)
+        nc.vector.tensor_tensor(out=frac[:], in0=turns[:], in1=whole[:], op=ALU.subtract)
+        sin_raw = const.tile([P, J, HALF], F32)
+        nc.scalar.activation(out=sin_raw[:], in_=frac[:], func=ACT.Sin, scale=2.0 * math.pi)
+        minus_abs = const.tile([P, J, HALF], F32)
+        nc.vector.scalar_tensor_tensor(
+            out=minus_abs[:].rearrange("p j d -> p (j d)"),
+            in0=frac[:].rearrange("p j d -> p (j d)"),
+            scalar=-1.0,
+            in1=frac[:].rearrange("p j d -> p (j d)"),
+            op0=ALU.mult,
+            op1=ALU.min,
+        )
+        cos_raw = const.tile([P, J, HALF], F32)
+        nc.scalar.activation(
+            out=cos_raw[:], in_=minus_abs[:], func=ACT.Sin, scale=2.0 * math.pi, bias=quarter_turn[:]
+        )
+        warm = const.tile([P, 1], F32)
+        nc.scalar.sqrt(out=warm[:], in_=one[:])
+
+        gain_own = const.tile([P, 2, 2, HALF], F32)
+        gain_other = const.tile([P, 2, 2, HALF], F32)
+        gamma_halves = gamma_bf[:].rearrange("p a (h d) -> p a h d", h=2)
+        nc.vector.tensor_copy(out=gain_own[:], in_=gamma_halves)
+        nc.vector.tensor_copy(out=gain_other[:, :, 0, :], in_=gamma_halves[:, :, 1, :])
+        nc.vector.tensor_scalar_mul(
+            out=gain_other[:, :, 1, :], in0=gamma_halves[:, :, 0, :], scalar1=-1.0
+        )
+        cos_gain = const.tile([P, J, 4, HALF], F32)
+        sin_gain = const.tile([P, J, 4, HALF], F32)
+
+        def fold_gains(row):
+            js = slice(CHUNK * row, CHUNK * (row + 1))
+            shape = [P, CHUNK, 4, HALF]
+            for table, raw, gain in ((cos_gain, cos_raw, gain_own), (sin_gain, sin_raw, gain_other)):
+                nc.vector.tensor_tensor(
+                    out=table[:, js, :, :],
+                    in0=raw[:, js, :].unsqueeze(2).to_broadcast(shape),
+                    in1=gain[:].rearrange("p a h d -> p (a h) d").unsqueeze(1).to_broadcast(shape),
+                    op=ALU.mult,
+                )
+
+        xt_banks, x_codes, x_scales, grouped_tiles = {}, {}, {}, {}
+        acc_banks, lengths, padded_lengths, inverse_norms = {}, {}, {}, {}
+        v_tiles, out_tiles, term_tiles = {}, {}, {}
+
+        def transpose_pair(g):
+            c, first_tile = g * PAIR // CHUNK, g * PAIR % CHUNK
+            words = x_tiles[c][:].bitcast(F32).rearrange("p j (s w u) -> p j s u w", s=PASSES, u=2)
+            xt_banks[g] = []
+            for i in range(PAIR):
+                xt = psum_xt.tile([P, PASSES, 2, P], F32, name="xt")
+                for s in range(PASSES):
+                    for u in range(2):
+                        nc.tensor.transpose(xt[:, s, u, :], words[:, first_tile + i, s, u, :], ident[:])
+                xt_banks[g].append(xt)
+
+        def regroup_pair(g):
+            grouped = quant.tile([P, PAIR, PASSES, P, 4], BF16, name="grouped", align_bytes=64)
+            for i in range(PAIR):
+                nc.scalar.copy(
+                    out=grouped[:, i].bitcast(F32),
+                    in_=xt_banks[g][i][:].rearrange("p s u t -> p s t u"),
+                )
+            grouped_tiles[g] = grouped
+            x_codes[g] = quant.tile([P, PAIR, PASSES, P], U32, name="codes", align_bytes=64)
+            x_scales[g] = quant.tile([P, PAIR, PASSES, P], U8, name="scales", align_bytes=64)
+
+        def quantise_tile(g, i):
+            nc.vector.quantize_mx(
+                out=x_codes[g][:, i].rearrange("p s t -> p (s t)").bitcast(FP8X4),
+                scales=x_scales[g][:, i].rearrange("p s t -> p (s t)"),
+                in_=grouped_tiles[g][:, i].rearrange("p s t e -> p (s t e)"),
+            )
+
+        def project_pair(g):
+            acc_banks[g] = []
+            for i in range(PAIR):
+                acc = psum_acc.tile([P, N_ALL], F32, name="acc")
+                for s in range(PASSES):
+                    nc.tensor.matmul_mx(
+                        out=acc[:],
+                        lhsT=x_codes[g][:, i, s, :].bitcast(FP8X4),
+                        lhsT_scale=x_scales[g][:, i, s, :],
+                        rhs=w_words[:, s, :].bitcast(FP8X4),
+                        rhs_scale=w_scales[:, s, :],
+                        start=(s == 0),
+                        stop=(s == PASSES - 1),
+                    )
+                acc_banks[g].append(acc)
+
+        def norms_and_v(g):
+            c, first_tile = g * PAIR // CHUNK, g * PAIR % CHUNK
+            if first_tile == 0:
+                v_tiles[c] = results.tile([P, CHUNK, HD], F32, name="v_sb")
+            squares = norm.tile([P, PAIR * ROPED, HD], BF16, name="squares")
+            sum_sq = norm.tile([P, PAIR * ROPED], F32, name="sum_sq")
+            for i in range(PAIR):
+                for h in range(ROPED):
+                    col = ROPED * i + h
+                    nc.scalar.activation(
+                        out=squares[:, col, :],
+                        in_=acc_banks[g][i][:, HD * h : HD * (h + 1)],
+                        func=ACT.Square,
+                        accum_out=sum_sq[:, col : col + 1],
+                    )
+            for i in range(PAIR):
+                nc.scalar.copy(out=v_tiles[c][:, first_tile + i, :], in_=acc_banks[g][i][:, HD * ROPED :])
+            length = norm.tile([P, PAIR * ROPED], F32, name="length")
+            nc.scalar.sqrt(out=length[:], in_=sum_sq[:])
+            lengths[g] = length
+
+        def add_eps(g):
+            padded = norm.tile([P, PAIR * ROPED], F32, name="padded")
+            nc.vector.tensor_scalar_add(out=padded[:], in0=lengths[g][:], scalar1=EPS)
+            padded_lengths[g] = padded
+
+        def invert(g):
+            inverse = norm.tile([P, PAIR * ROPED], F32, name="inverse")
+            nc.vector.reciprocal(out=inverse[:], in_=padded_lengths[g][:])
+            inverse_norms[g] = inverse
+
+        def rope_products(g):
+            j0 = CHUNK * (g * PAIR // CHUNK // B) + g * PAIR % CHUNK
+            own = terms.tile([P, ROPED, PAIR, HD], F32, name="own")
+            other = terms.tile([P, ROPED, PAIR, HD], F32, name="other")
+            for i in range(PAIR):
+                for h in range(ROPED):
+                    which = 0 if h < Q_HEADS else 1
+                    col = ROPED * i + h
+                    for term, table in ((own, cos_gain), (other, sin_gain)):
+                        nc.vector.scalar_tensor_tensor(
+                            out=term[:, h, i, :],
+                            in0=acc_banks[g][i][:, HD * h : HD * (h + 1)],
+                            scalar=inverse_norms[g][:, col : col + 1],
+                            in1=table[:, j0 + i, 2 * which : 2 * which + 2, :].rearrange("p h d -> p (h d)"),
+                            op0=ALU.mult,
+                            op1=ALU.mult,
+                        )
+            term_tiles[g] = (own, other)
+
+        def add_terms(g):
+            c, first_tile = g * PAIR // CHUNK, g * PAIR % CHUNK
+            if first_tile == 0:
+                out_tiles[c] = results.tile([P, ROPED, CHUNK, HD], F32, name="qk_sb")
+            own, other = term_tiles[g]
+            tiles = slice(first_tile, first_tile + PAIR)
+            for half in range(2):
+                here = slice(HALF * half, HALF * (half + 1))
+                there = slice(HALF * (1 - half), HALF * (2 - half))
+                nc.gpsimd.tensor_tensor(
+                    out=out_tiles[c][:, :, tiles, here],
+                    in0=own[:, :, :, here],
+                    in1=other[:, :, :, there],
+                    op=ALU.add,
+                )
+
+        def store_chunk(c):
+            j0, b = CHUNK * (c // B), c % B
+            js = slice(j0, j0 + CHUNK)
+            nc.sync.dma_start(out=v_view[b, :, 0, js, :], in_=v_tiles[c][:])
+            nc.sync.dma_start(out=q_view[b, :, :, js, :], in_=out_tiles[c][:, 0:Q_HEADS, :, :])
+            nc.sync.dma_start(out=k_view[b, :, 0, js, :], in_=out_tiles[c][:, Q_HEADS, :, :])
+
+        pairs_per_row = B * CHUNK // PAIR
+        for g in range(-2, PAIRS):
+            ahead, nxt = g + 2, g + 1
+            if ahead < PAIRS:
+                transpose_pair(ahead)
+                regroup_pair(ahead)
+                if (ahead + 1) * PAIR % CHUNK == 0 and ahead * PAIR // CHUNK + X_BUFS < CHUNKS:
+                    load_chunk(ahead * PAIR // CHUNK + X_BUFS)
+            if 0 <= nxt < PAIRS:
+                project_pair(nxt)
+                norms_and_v(nxt)
+            if 0 <= nxt < PAIRS and nxt % pairs_per_row == 0:
+                fold_gains(nxt // pairs_per_row)
+            if g >= 0:
+                rope_products(g)
+                add_terms(g)
+                if (g + 1) * PAIR % CHUNK == 0:
+                    store_chunk(g * PAIR // CHUNK)
+            if 0 <= nxt < PAIRS:
+                add_eps(nxt)
+            if ahead < PAIRS:
+                quantise_tile(ahead, 0)
+            if 0 <= nxt < PAIRS:
+                invert(nxt)
+            if ahead < PAIRS:
+                quantise_tile(ahead, 1)

@@ -290,7 +290,7 @@ def tile_gqaattention_pa_t_kernel(
             for half in range(2):
                 here = slice(HALF * half, HALF * (half + 1))
                 there = slice(HALF * (1 - half), HALF * (2 - half))
-                nc.gpsimd.tensor_tensor(
+                nc.vector.tensor_tensor(
                     out=out_tiles[c][:, :, tiles, here],
                     in0=own[:, :, :, here],
                     in1=other[:, :, :, there],
@@ -319,9 +319,6 @@ def tile_gqaattention_pa_t_kernel(
                 fold_gains(nxt // pairs_per_row)
             if g >= 0:
                 rope_products(g)
-                add_terms(g)
-                if (g + 1) * PAIR % CHUNK == 0:
-                    store_chunk(g * PAIR // CHUNK)
             if 0 <= nxt < PAIRS:
                 add_eps(nxt)
             if ahead < PAIRS:
@@ -330,3 +327,7 @@ def tile_gqaattention_pa_t_kernel(
                 invert(nxt)
             if ahead < PAIRS:
                 quantise_tile(ahead, 1)
+            if g >= 0:
+                add_terms(g)
+                if (g + 1) * PAIR % CHUNK == 0:
+                    store_chunk(g * PAIR // CHUNK)

@@ -31,6 +31,9 @@ PAIR = 2
 CHUNKS = B * J // CHUNK
 PAIRS = CHUNKS * CHUNK // PAIR
 X_BUFS = 4
+PROJECT_AHEAD = 2
+QUANTISE_AHEAD = 4
+TRANSPOSE_AHEAD = 5
 ROUND_MAGIC = 1.5 * 2.0**23
 
 FLOPS = 2 * B * T * D * N_ALL
@@ -56,12 +59,12 @@ def tile_gqaattention_pa_t_kernel(
         ctx.enter_context(tc.manual_schedule())
         const = ctx.enter_context(tc.tile_pool(name="const", bufs=1))
         x_pool = ctx.enter_context(tc.tile_pool(name="x", bufs=X_BUFS))
-        quant = ctx.enter_context(tc.tile_pool(name="quant", bufs=3))
-        norm = ctx.enter_context(tc.tile_pool(name="norm", bufs=3))
+        quant = ctx.enter_context(tc.tile_pool(name="quant", bufs=4))
+        norm = ctx.enter_context(tc.tile_pool(name="norm", bufs=4))
         terms = ctx.enter_context(tc.tile_pool(name="terms", bufs=3))
-        results = ctx.enter_context(tc.tile_pool(name="results", bufs=3))
-        psum_xt = ctx.enter_context(tc.psum_pool(name="psum_xt", bufs=2 * PAIR))
-        psum_acc = ctx.enter_context(tc.psum_pool(name="psum_acc", bufs=2 * PAIR))
+        results = ctx.enter_context(tc.tile_pool(name="results", bufs=6))
+        psum_xt = ctx.enter_context(tc.psum_pool(name="psum_xt", bufs=PAIR))
+        psum_acc = ctx.enter_context(tc.psum_pool(name="psum_acc", bufs=(PROJECT_AHEAD + 1) * PAIR))
 
         x_view = x.rearrange("b (p j) k -> b p j k", j=J)
         q_view = out_0.rearrange("b h (p j) d -> b p h j d", j=J)
@@ -160,25 +163,25 @@ def tile_gqaattention_pa_t_kernel(
         warm = const.tile([P, 1], F32)
         nc.scalar.sqrt(out=warm[:], in_=one[:])
 
-        gain_own = const.tile([P, 2, 2, HALF], F32)
-        gain_other = const.tile([P, 2, 2, HALF], F32)
+        gain = const.tile([P, 2, 2, HALF], F32)
+        signed_gain = const.tile([P, 2, 2, HALF], F32)
         gamma_halves = gamma_bf[:].rearrange("p a (h d) -> p a h d", h=2)
-        nc.vector.tensor_copy(out=gain_own[:], in_=gamma_halves)
-        nc.vector.tensor_copy(out=gain_other[:, :, 0, :], in_=gamma_halves[:, :, 1, :])
+        nc.vector.tensor_copy(out=gain[:], in_=gamma_halves)
         nc.vector.tensor_scalar_mul(
-            out=gain_other[:, :, 1, :], in0=gamma_halves[:, :, 0, :], scalar1=-1.0
+            out=signed_gain[:, :, 0, :], in0=gamma_halves[:, :, 0, :], scalar1=-1.0
         )
+        nc.vector.tensor_copy(out=signed_gain[:, :, 1, :], in_=gamma_halves[:, :, 1, :])
         cos_gain = const.tile([P, J, 4, HALF], F32)
         sin_gain = const.tile([P, J, 4, HALF], F32)
 
         def fold_gains(row):
             js = slice(CHUNK * row, CHUNK * (row + 1))
             shape = [P, CHUNK, 4, HALF]
-            for table, raw, gain in ((cos_gain, cos_raw, gain_own), (sin_gain, sin_raw, gain_other)):
+            for table, raw, factor in ((sin_gain, sin_raw, signed_gain), (cos_gain, cos_raw, gain)):
                 nc.vector.tensor_tensor(
                     out=table[:, js, :, :],
                     in0=raw[:, js, :].unsqueeze(2).to_broadcast(shape),
-                    in1=gain[:].rearrange("p a h d -> p (a h) d").unsqueeze(1).to_broadcast(shape),
+                    in1=factor[:].rearrange("p a h d -> p (a h) d").unsqueeze(1).to_broadcast(shape),
                     op=ALU.mult,
                 )
 
@@ -232,9 +235,7 @@ def tile_gqaattention_pa_t_kernel(
                 acc_banks[g].append(acc)
 
         def norms_and_v(g):
-            c, first_tile = g * PAIR // CHUNK, g * PAIR % CHUNK
-            if first_tile == 0:
-                v_tiles[c] = results.tile([P, CHUNK, HD], F32, name="v_sb")
+            v_tiles[g] = results.tile([P, PAIR, HD], F32, name="v_sb")
             squares = norm.tile([P, PAIR * ROPED, HD], BF16, name="squares")
             sum_sq = norm.tile([P, PAIR * ROPED], F32, name="sum_sq")
             for i in range(PAIR):
@@ -247,7 +248,7 @@ def tile_gqaattention_pa_t_kernel(
                         accum_out=sum_sq[:, col : col + 1],
                     )
             for i in range(PAIR):
-                nc.scalar.copy(out=v_tiles[c][:, first_tile + i, :], in_=acc_banks[g][i][:, HD * ROPED :])
+                nc.scalar.copy(out=v_tiles[g][:, i, :], in_=acc_banks[g][i][:, HD * ROPED :])
             length = norm.tile([P, PAIR * ROPED], F32, name="length")
             nc.scalar.sqrt(out=length[:], in_=sum_sq[:])
             lengths[g] = length
@@ -262,72 +263,76 @@ def tile_gqaattention_pa_t_kernel(
             nc.vector.reciprocal(out=inverse[:], in_=padded_lengths[g][:])
             inverse_norms[g] = inverse
 
-        def rope_products(g):
-            j0 = CHUNK * (g * PAIR // CHUNK // B) + g * PAIR % CHUNK
-            own = terms.tile([P, ROPED, PAIR, HD], F32, name="own")
-            other = terms.tile([P, ROPED, PAIR, HD], F32, name="other")
-            for i in range(PAIR):
-                for h in range(ROPED):
-                    which = 0 if h < Q_HEADS else 1
-                    col = ROPED * i + h
-                    for term, table in ((own, cos_gain), (other, sin_gain)):
-                        nc.vector.scalar_tensor_tensor(
-                            out=term[:, h, i, :],
-                            in0=acc_banks[g][i][:, HD * h : HD * (h + 1)],
-                            scalar=inverse_norms[g][:, col : col + 1],
-                            in1=table[:, j0 + i, 2 * which : 2 * which + 2, :].rearrange("p h d -> p (h d)"),
-                            op0=ALU.mult,
-                            op1=ALU.mult,
-                        )
-            term_tiles[g] = (own, other)
+        def rope_products(g, i):
+            j = CHUNK * (g * PAIR // CHUNK // B) + g * PAIR % CHUNK + i
+            if i == 0:
+                term_tiles[g] = (
+                    terms.tile([P, ROPED, PAIR, HD], F32, name="own"),
+                    terms.tile([P, ROPED, PAIR, HD], F32, name="other"),
+                )
+            own, other = term_tiles[g]
+            for h in range(ROPED):
+                which = 0 if h < Q_HEADS else 1
+                u = acc_banks[g][i][:, HD * h : HD * (h + 1)]
+                inverse = inverse_norms[g][:, ROPED * i + h : ROPED * i + h + 1]
+                nc.vector.scalar_tensor_tensor(
+                    out=own[:, h, i, :],
+                    in0=u,
+                    scalar=inverse,
+                    in1=cos_gain[:, j, 2 * which : 2 * which + 2, :].rearrange("p h d -> p (h d)"),
+                    op0=ALU.mult,
+                    op1=ALU.mult,
+                )
+                for half in range(2):
+                    nc.vector.scalar_tensor_tensor(
+                        out=other[:, h, i, HALF * half : HALF * (half + 1)],
+                        in0=u[:, HALF * (1 - half) : HALF * (2 - half)],
+                        scalar=inverse,
+                        in1=sin_gain[:, j, 2 * which + half, :],
+                        op0=ALU.mult,
+                        op1=ALU.mult,
+                    )
 
         def add_terms(g):
-            c, first_tile = g * PAIR // CHUNK, g * PAIR % CHUNK
-            if first_tile == 0:
-                out_tiles[c] = results.tile([P, ROPED, CHUNK, HD], F32, name="qk_sb")
             own, other = term_tiles[g]
-            tiles = slice(first_tile, first_tile + PAIR)
-            for half in range(2):
-                here = slice(HALF * half, HALF * (half + 1))
-                there = slice(HALF * (1 - half), HALF * (2 - half))
-                nc.vector.tensor_tensor(
-                    out=out_tiles[c][:, :, tiles, here],
-                    in0=own[:, :, :, here],
-                    in1=other[:, :, :, there],
-                    op=ALU.add,
-                )
+            out_tiles[g] = results.tile([P, ROPED, PAIR, HD], F32, name="qk_sb")
+            nc.gpsimd.tensor_tensor(out=out_tiles[g][:], in0=own[:], in1=other[:], op=ALU.add)
 
-        def store_chunk(c):
-            j0, b = CHUNK * (c // B), c % B
-            js = slice(j0, j0 + CHUNK)
-            nc.sync.dma_start(out=v_view[b, :, 0, js, :], in_=v_tiles[c][:])
-            nc.sync.dma_start(out=q_view[b, :, :, js, :], in_=out_tiles[c][:, 0:Q_HEADS, :, :])
-            nc.sync.dma_start(out=k_view[b, :, 0, js, :], in_=out_tiles[c][:, Q_HEADS, :, :])
+        def store_pair(g):
+            c, first_tile = g * PAIR // CHUNK, g * PAIR % CHUNK
+            b = c % B
+            js = slice(CHUNK * (c // B) + first_tile, CHUNK * (c // B) + first_tile + PAIR)
+            nc.sync.dma_start(out=v_view[b, :, 0, js, :], in_=v_tiles[g][:])
+            nc.sync.dma_start(out=q_view[b, :, :, js, :], in_=out_tiles[g][:, 0:Q_HEADS, :, :])
+            nc.sync.dma_start(out=k_view[b, :, 0, js, :], in_=out_tiles[g][:, Q_HEADS, :, :])
 
-        pairs_per_row = B * CHUNK // PAIR
-        for g in range(-2, PAIRS):
-            ahead, nxt = g + 2, g + 1
-            if ahead < PAIRS:
-                transpose_pair(ahead)
-                regroup_pair(ahead)
-                if (ahead + 1) * PAIR % CHUNK == 0 and ahead * PAIR // CHUNK + X_BUFS < CHUNKS:
-                    load_chunk(ahead * PAIR // CHUNK + X_BUFS)
-            if 0 <= nxt < PAIRS:
-                project_pair(nxt)
-                norms_and_v(nxt)
-            if 0 <= nxt < PAIRS and nxt % pairs_per_row == 0:
-                fold_gains(nxt // pairs_per_row)
-            if g >= 0:
-                rope_products(g)
-            if 0 <= nxt < PAIRS:
-                add_eps(nxt)
-            if ahead < PAIRS:
-                quantise_tile(ahead, 0)
-            if 0 <= nxt < PAIRS:
-                invert(nxt)
-            if ahead < PAIRS:
-                quantise_tile(ahead, 1)
-            if g >= 0:
+
+        def exists(pair):
+            return 0 <= pair < PAIRS
+
+        for g in range(-TRANSPOSE_AHEAD, PAIRS):
+            if exists(g + PROJECT_AHEAD):
+                project_pair(g + PROJECT_AHEAD)
+                norms_and_v(g + PROJECT_AHEAD)
+            if exists(g + TRANSPOSE_AHEAD):
+                transpose_pair(g + TRANSPOSE_AHEAD)
+                regroup_pair(g + TRANSPOSE_AHEAD)
+                c = (g + TRANSPOSE_AHEAD) * PAIR // CHUNK
+                if (g + TRANSPOSE_AHEAD + 1) * PAIR % CHUNK == 0 and c + X_BUFS < CHUNKS:
+                    load_chunk(c + X_BUFS)
+            if exists(g):
+                rope_products(g, 0)
+            if exists(g + 1):
+                invert(g + 1)
+            if exists(g):
+                rope_products(g, 1)
+            if exists(g + QUANTISE_AHEAD):
+                quantise_tile(g + QUANTISE_AHEAD, 0)
+                quantise_tile(g + QUANTISE_AHEAD, 1)
+            if g + TRANSPOSE_AHEAD < J // CHUNK:
+                fold_gains(g + TRANSPOSE_AHEAD)
+            if exists(g + PROJECT_AHEAD):
+                add_eps(g + PROJECT_AHEAD)
+            if exists(g):
                 add_terms(g)
-                if (g + 1) * PAIR % CHUNK == 0:
-                    store_chunk(g * PAIR // CHUNK)
+                store_pair(g)

@@ -80,6 +80,7 @@ def tile_gqaattention_pa_t_kernel(
             x_tiles[c] = x_sb
 
         load_chunk(0)
+        load_chunk(1)
         gamma_bf = const.tile([P, 2, HD], BF16)
         nc.sync.dma_start(out=gamma_bf[:, 0, :], in_=gamma_q.partition_broadcast(P))
         nc.sync.dma_start(out=gamma_bf[:, 1, :], in_=gamma_k.partition_broadcast(P))
@@ -103,7 +104,7 @@ def tile_gqaattention_pa_t_kernel(
                 in_=words.rearrange("g p n t -> p g (n t)").bitcast(I32),
             )
 
-        for c in range(1, X_BUFS):
+        for c in range(2, X_BUFS):
             load_chunk(c)
 
         position_i = const.tile([P, J], I32)
@@ -115,25 +116,20 @@ def tile_gqaattention_pa_t_kernel(
         nc.vector.memset(one[:], 1.0)
         quarter_turn = const.tile([P, 1], F32)
         nc.vector.tensor_scalar_mul(out=quarter_turn[:], in0=one[:], scalar1=math.pi / 2)
-        freq = const.tile([P, HALF], F32)
-        nc.vector.tensor_scalar_mul(out=freq[:, 0:1], in0=one[:], scalar1=1.0 / (2.0 * math.pi))
-        width = 1
-        while width < HALF:
-            nc.vector.tensor_scalar_mul(
-                out=freq[:, width : 2 * width],
-                in0=freq[:, 0:width],
-                scalar1=ROPE_BASE ** (-width / HALF),
-            )
-            width *= 2
         position = const.tile([P, J], F32)
         nc.vector.tensor_copy(out=position[:], in_=position_i[:])
         turns = const.tile([P, J, HALF], F32)
-        nc.vector.tensor_tensor(
-            out=turns[:],
-            in0=position[:].unsqueeze(2).to_broadcast([P, J, HALF]),
-            in1=freq[:].unsqueeze(1).to_broadcast([P, J, HALF]),
-            op=ALU.mult,
+        nc.vector.tensor_scalar_mul(
+            out=turns[:, :, 0:1], in0=position[:].unsqueeze(2), scalar1=1.0 / (2.0 * math.pi)
         )
+        width = 1
+        while width < HALF:
+            nc.vector.tensor_scalar_mul(
+                out=turns[:, :, width : 2 * width],
+                in0=turns[:, :, 0:width],
+                scalar1=ROPE_BASE ** (-width / HALF),
+            )
+            width *= 2
         whole = const.tile([P, J, HALF], F32)
         nc.vector.tensor_scalar(
             out=whole[:],
@@ -145,8 +141,8 @@ def tile_gqaattention_pa_t_kernel(
         )
         frac = const.tile([P, J, HALF], F32)
         nc.vector.tensor_tensor(out=frac[:], in0=turns[:], in1=whole[:], op=ALU.subtract)
-        sin_raw = const.tile([P, J, HALF], F32)
-        nc.scalar.activation(out=sin_raw[:], in_=frac[:], func=ACT.Sin, scale=2.0 * math.pi)
+        cos_sin = const.tile([P, J, 2, HALF], F32)
+        nc.scalar.activation(out=cos_sin[:, :, 1, :], in_=frac[:], func=ACT.Sin, scale=2.0 * math.pi)
         minus_abs = const.tile([P, J, HALF], F32)
         nc.vector.scalar_tensor_tensor(
             out=minus_abs[:].rearrange("p j d -> p (j d)"),
@@ -156,34 +152,32 @@ def tile_gqaattention_pa_t_kernel(
             op0=ALU.mult,
             op1=ALU.min,
         )
-        cos_raw = const.tile([P, J, HALF], F32)
         nc.scalar.activation(
-            out=cos_raw[:], in_=minus_abs[:], func=ACT.Sin, scale=2.0 * math.pi, bias=quarter_turn[:]
+            out=cos_sin[:, :, 0, :],
+            in_=minus_abs[:],
+            func=ACT.Sin,
+            scale=2.0 * math.pi,
+            bias=quarter_turn[:],
         )
         warm = const.tile([P, 1], F32)
         nc.scalar.sqrt(out=warm[:], in_=one[:])
 
-        gain = const.tile([P, 2, 2, HALF], F32)
-        signed_gain = const.tile([P, 2, 2, HALF], F32)
+        gain = const.tile([P, 2, 2, 2, HALF], F32)
         gamma_halves = gamma_bf[:].rearrange("p a (h d) -> p a h d", h=2)
-        nc.vector.tensor_copy(out=gain[:], in_=gamma_halves)
-        nc.vector.tensor_scalar_mul(
-            out=signed_gain[:, :, 0, :], in0=gamma_halves[:, :, 0, :], scalar1=-1.0
-        )
-        nc.vector.tensor_copy(out=signed_gain[:, :, 1, :], in_=gamma_halves[:, :, 1, :])
-        cos_gain = const.tile([P, J, 4, HALF], F32)
-        sin_gain = const.tile([P, J, 4, HALF], F32)
+        nc.vector.tensor_copy(out=gain[:, :, :, 0, :], in_=gamma_halves)
+        nc.vector.tensor_copy(out=gain[:, :, 0, 1, :], in_=gamma_halves[:, :, 1, :])
+        nc.vector.tensor_scalar_mul(out=gain[:, :, 1, 1, :], in0=gamma_halves[:, :, 0, :], scalar1=-1.0)
+        table = const.tile([P, J, 2, 2, 2, HALF], F32)
 
         def fold_gains(row):
             js = slice(CHUNK * row, CHUNK * (row + 1))
-            shape = [P, CHUNK, 4, HALF]
-            for table, raw, factor in ((sin_gain, sin_raw, signed_gain), (cos_gain, cos_raw, gain)):
-                nc.vector.tensor_tensor(
-                    out=table[:, js, :, :],
-                    in0=raw[:, js, :].unsqueeze(2).to_broadcast(shape),
-                    in1=factor[:].rearrange("p a h d -> p (a h) d").unsqueeze(1).to_broadcast(shape),
-                    op=ALU.mult,
-                )
+            shape = [P, CHUNK, 4, HD]
+            nc.vector.tensor_tensor(
+                out=table[:, js].rearrange("p j a h r d -> p j (a h) (r d)"),
+                in0=cos_sin[:, js].rearrange("p j r d -> p j (r d)").unsqueeze(2).to_broadcast(shape),
+                in1=gain[:].rearrange("p a h r d -> p (a h) (r d)").unsqueeze(1).to_broadcast(shape),
+                op=ALU.mult,
+            )
 
         xt_banks, x_codes, x_scales, grouped_tiles = {}, {}, {}, {}
         acc_banks, lengths, padded_lengths, inverse_norms = {}, {}, {}, {}
@@ -266,45 +260,38 @@ def tile_gqaattention_pa_t_kernel(
         def rope_products(g, i):
             j = CHUNK * (g * PAIR // CHUNK // B) + g * PAIR % CHUNK + i
             if i == 0:
-                term_tiles[g] = (
-                    terms.tile([P, ROPED, PAIR, HD], F32, name="own"),
-                    terms.tile([P, ROPED, PAIR, HD], F32, name="other"),
-                )
-            own, other = term_tiles[g]
+                term_tiles[g] = terms.tile([P, ROPED, PAIR, 4, HALF], F32, name="terms")
             for h in range(ROPED):
                 which = 0 if h < Q_HEADS else 1
-                u = acc_banks[g][i][:, HD * h : HD * (h + 1)]
-                inverse = inverse_norms[g][:, ROPED * i + h : ROPED * i + h + 1]
-                nc.vector.scalar_tensor_tensor(
-                    out=own[:, h, i, :],
-                    in0=u,
-                    scalar=inverse,
-                    in1=cos_gain[:, j, 2 * which : 2 * which + 2, :].rearrange("p h d -> p (h d)"),
-                    op0=ALU.mult,
-                    op1=ALU.mult,
-                )
-                for half in range(2):
+                for half, rows in ((0, slice(0, 4, 3)), (1, slice(1, 3))):
+                    first = HD * h + HALF * half
                     nc.vector.scalar_tensor_tensor(
-                        out=other[:, h, i, HALF * half : HALF * (half + 1)],
-                        in0=u[:, HALF * (1 - half) : HALF * (2 - half)],
-                        scalar=inverse,
-                        in1=sin_gain[:, j, 2 * which + half, :],
+                        out=term_tiles[g][:, h, i, rows, :],
+                        in0=acc_banks[g][i][:, first : first + HALF].unsqueeze(1).to_broadcast([P, 2, HALF]),
+                        scalar=inverse_norms[g][:, ROPED * i + h : ROPED * i + h + 1],
+                        in1=table[:, j, which, half, :, :],
                         op0=ALU.mult,
                         op1=ALU.mult,
                     )
 
         def add_terms(g):
-            own, other = term_tiles[g]
-            out_tiles[g] = results.tile([P, ROPED, PAIR, HD], F32, name="qk_sb")
-            nc.gpsimd.tensor_tensor(out=out_tiles[g][:], in0=own[:], in1=other[:], op=ALU.add)
+            out_tiles[g] = results.tile([P, ROPED, PAIR, 2, HALF], F32, name="qk_sb")
+            engine = nc.gpsimd if g < PAIRS - 1 else nc.vector
+            engine.tensor_tensor(
+                out=out_tiles[g][:],
+                in0=term_tiles[g][:, :, :, 0:2, :],
+                in1=term_tiles[g][:, :, :, 2:4, :],
+                op=ALU.add,
+            )
 
         def store_pair(g):
             c, first_tile = g * PAIR // CHUNK, g * PAIR % CHUNK
             b = c % B
             js = slice(CHUNK * (c // B) + first_tile, CHUNK * (c // B) + first_tile + PAIR)
             nc.sync.dma_start(out=v_view[b, :, 0, js, :], in_=v_tiles[g][:])
-            nc.sync.dma_start(out=q_view[b, :, :, js, :], in_=out_tiles[g][:, 0:Q_HEADS, :, :])
-            nc.sync.dma_start(out=k_view[b, :, 0, js, :], in_=out_tiles[g][:, Q_HEADS, :, :])
+            qk = out_tiles[g][:].rearrange("p h i a d -> p h i (a d)")
+            nc.sync.dma_start(out=q_view[b, :, :, js, :], in_=qk[:, 0:Q_HEADS, :, :])
+            nc.sync.dma_start(out=k_view[b, :, 0, js, :], in_=qk[:, Q_HEADS, :, :])
 
 
         def exists(pair):

@@ -141,8 +141,11 @@ def tile_gqaattention_pa_t_kernel(
         )
         frac = const.tile([P, J, HALF], F32)
         nc.vector.tensor_tensor(out=frac[:], in0=turns[:], in1=whole[:], op=ALU.subtract)
-        cos_sin = const.tile([P, J, 2, HALF], F32)
-        nc.scalar.activation(out=cos_sin[:, :, 1, :], in_=frac[:], func=ACT.Sin, scale=2.0 * math.pi)
+        cos_sin = const.tile([P, J, 4, HALF], F32)
+        twice = [P, J, 2, HALF]
+        nc.scalar.activation(
+            out=cos_sin[:, :, 1:3, :], in_=frac[:].unsqueeze(2).to_broadcast(twice), func=ACT.Sin, scale=2.0 * math.pi
+        )
         minus_abs = const.tile([P, J, HALF], F32)
         nc.vector.scalar_tensor_tensor(
             out=minus_abs[:].rearrange("p j d -> p (j d)"),
@@ -153,8 +156,8 @@ def tile_gqaattention_pa_t_kernel(
             op1=ALU.min,
         )
         nc.scalar.activation(
-            out=cos_sin[:, :, 0, :],
-            in_=minus_abs[:],
+            out=cos_sin[:, :, 0:4:3, :],
+            in_=minus_abs[:].unsqueeze(2).to_broadcast(twice),
             func=ACT.Sin,
             scale=2.0 * math.pi,
             bias=quarter_turn[:],
@@ -165,17 +168,17 @@ def tile_gqaattention_pa_t_kernel(
         gain = const.tile([P, 2, 2, 2, HALF], F32)
         gamma_halves = gamma_bf[:].rearrange("p a (h d) -> p a h d", h=2)
         nc.vector.tensor_copy(out=gain[:, :, :, 0, :], in_=gamma_halves)
-        nc.vector.tensor_copy(out=gain[:, :, 0, 1, :], in_=gamma_halves[:, :, 1, :])
-        nc.vector.tensor_scalar_mul(out=gain[:, :, 1, 1, :], in0=gamma_halves[:, :, 0, :], scalar1=-1.0)
+        nc.vector.tensor_copy(out=gain[:, :, 1, 1, :], in_=gamma_halves[:, :, 1, :])
+        nc.vector.tensor_scalar_mul(out=gain[:, :, 0, 1, :], in0=gamma_halves[:, :, 0, :], scalar1=-1.0)
         table = const.tile([P, J, 2, 2, 2, HALF], F32)
 
         def fold_gains(row):
             js = slice(CHUNK * row, CHUNK * (row + 1))
-            shape = [P, CHUNK, 4, HD]
+            shape = [P, CHUNK, 2, 2 * HD]
             nc.vector.tensor_tensor(
-                out=table[:, js].rearrange("p j a h r d -> p j (a h) (r d)"),
+                out=table[:, js].rearrange("p j a h r d -> p j a (h r d)"),
                 in0=cos_sin[:, js].rearrange("p j r d -> p j (r d)").unsqueeze(2).to_broadcast(shape),
-                in1=gain[:].rearrange("p a h r d -> p (a h) (r d)").unsqueeze(1).to_broadcast(shape),
+                in1=gain[:].rearrange("p a h r d -> p a (h r d)").unsqueeze(1).to_broadcast(shape),
                 op=ALU.mult,
             )
 
@@ -260,27 +263,25 @@ def tile_gqaattention_pa_t_kernel(
         def rope_products(g, i):
             j = CHUNK * (g * PAIR // CHUNK // B) + g * PAIR % CHUNK + i
             if i == 0:
-                term_tiles[g] = terms.tile([P, ROPED, PAIR, 4, HALF], F32, name="terms")
+                term_tiles[g] = terms.tile([P, ROPED, PAIR, 2, 2, HALF], F32, name="terms")
             for h in range(ROPED):
                 which = 0 if h < Q_HEADS else 1
-                for half, rows in ((0, slice(0, 4, 3)), (1, slice(1, 3))):
-                    first = HD * h + HALF * half
-                    nc.vector.scalar_tensor_tensor(
-                        out=term_tiles[g][:, h, i, rows, :],
-                        in0=acc_banks[g][i][:, first : first + HALF].unsqueeze(1).to_broadcast([P, 2, HALF]),
-                        scalar=inverse_norms[g][:, ROPED * i + h : ROPED * i + h + 1],
-                        in1=table[:, j, which, half, :, :],
-                        op0=ALU.mult,
-                        op1=ALU.mult,
-                    )
+                nc.vector.scalar_tensor_tensor(
+                    out=term_tiles[g][:, h, i, :, :, :].rearrange("p r a d -> p r (a d)"),
+                    in0=acc_banks[g][i][:, HD * h : HD * (h + 1)].unsqueeze(1).to_broadcast([P, 2, HD]),
+                    scalar=inverse_norms[g][:, ROPED * i + h : ROPED * i + h + 1],
+                    in1=table[:, j, which, :, :, :].rearrange("p r a d -> p r (a d)"),
+                    op0=ALU.mult,
+                    op1=ALU.mult,
+                )
 
         def add_terms(g):
             out_tiles[g] = results.tile([P, ROPED, PAIR, 2, HALF], F32, name="qk_sb")
             engine = nc.gpsimd if g < PAIRS - 1 else nc.vector
             engine.tensor_tensor(
                 out=out_tiles[g][:],
-                in0=term_tiles[g][:, :, :, 0:2, :],
-                in1=term_tiles[g][:, :, :, 2:4, :],
+                in0=term_tiles[g][:, :, :, :, 0, :],
+                in1=term_tiles[g][:, :, :, :, 1, :],
                 op=ALU.add,
             )
 

@@ -76,11 +76,16 @@ def tile_gqaattention_pa_t_kernel(
         def load_chunk(c):
             j0, b = CHUNK * (c // B), c % B
             x_sb = x_pool.tile([P, CHUNK, D], BF16, name="x_sb")
-            nc.sync.dma_start(out=x_sb[:], in_=x_view[b, :, j0 : j0 + CHUNK, :])
+            pieces = CHUNK // PAIR if c == 0 else 1
+            width = CHUNK // pieces
+            for first_tile in range(0, CHUNK, width):
+                nc.sync.dma_start(
+                    out=x_sb[:, first_tile : first_tile + width, :],
+                    in_=x_view[b, :, j0 + first_tile : j0 + first_tile + width, :],
+                )
             x_tiles[c] = x_sb
 
         load_chunk(0)
-        load_chunk(1)
         gamma_bf = const.tile([P, 2, HD], BF16)
         nc.sync.dma_start(out=gamma_bf[:, 0, :], in_=gamma_q.partition_broadcast(P))
         nc.sync.dma_start(out=gamma_bf[:, 1, :], in_=gamma_k.partition_broadcast(P))
@@ -88,6 +93,10 @@ def tile_gqaattention_pa_t_kernel(
         w_words = const.tile([P, PASSES, N_ALL], U32, align_bytes=64)
         w_scales = const.tile([P, PASSES, N_ALL], U8, align_bytes=64)
         nc.vector.memset(w_scales[:].bitcast(I32), 0)
+        one = const.tile([P, 1], F32)
+        nc.vector.memset(one[:], 1.0)
+        warm = const.tile([P, 2], F32)
+        nc.scalar.activation(out=warm[:, 0:1], in_=one[:], func=ACT.Sin)
         first = 0
         for words, scales in ((wq_words, wq_scales), (wk_words, wk_scales), (wv_words, wv_scales)):
             cols = slice(first, first + words.shape[2])
@@ -104,7 +113,7 @@ def tile_gqaattention_pa_t_kernel(
                 in_=words.rearrange("g p n t -> p g (n t)").bitcast(I32),
             )
 
-        for c in range(2, X_BUFS):
+        for c in range(1, X_BUFS):
             load_chunk(c)
 
         position_i = const.tile([P, J], I32)
@@ -112,58 +121,67 @@ def tile_gqaattention_pa_t_kernel(
         ident = const.tile([P, P], F32)
         make_identity(nc, ident[:])
 
-        one = const.tile([P, 1], F32)
-        nc.vector.memset(one[:], 1.0)
         quarter_turn = const.tile([P, 1], F32)
         nc.vector.tensor_scalar_mul(out=quarter_turn[:], in0=one[:], scalar1=math.pi / 2)
         position = const.tile([P, J], F32)
         nc.vector.tensor_copy(out=position[:], in_=position_i[:])
-        turns = const.tile([P, J, HALF], F32)
-        nc.vector.tensor_scalar_mul(
-            out=turns[:, :, 0:1], in0=position[:].unsqueeze(2), scalar1=1.0 / (2.0 * math.pi)
-        )
+        per_position = const.tile([P, HALF], F32)
+        nc.vector.tensor_scalar_mul(out=per_position[:, 0:1], in0=one[:], scalar1=1.0 / (2.0 * math.pi))
         width = 1
         while width < HALF:
             nc.vector.tensor_scalar_mul(
-                out=turns[:, :, width : 2 * width],
-                in0=turns[:, :, 0:width],
+                out=per_position[:, width : 2 * width],
+                in0=per_position[:, 0:width],
                 scalar1=ROPE_BASE ** (-width / HALF),
             )
             width *= 2
+        turns = const.tile([P, J, HALF], F32)
         whole = const.tile([P, J, HALF], F32)
-        nc.vector.tensor_scalar(
-            out=whole[:],
-            in0=turns[:],
-            scalar1=ROUND_MAGIC,
-            scalar2=ROUND_MAGIC,
-            op0=ALU.add,
-            op1=ALU.subtract,
-        )
         frac = const.tile([P, J, HALF], F32)
-        nc.vector.tensor_tensor(out=frac[:], in0=turns[:], in1=whole[:], op=ALU.subtract)
-        cos_sin = const.tile([P, J, 4, HALF], F32)
-        twice = [P, J, 2, HALF]
-        nc.scalar.activation(
-            out=cos_sin[:, :, 1:3, :], in_=frac[:].unsqueeze(2).to_broadcast(twice), func=ACT.Sin, scale=2.0 * math.pi
-        )
         minus_abs = const.tile([P, J, HALF], F32)
-        nc.vector.scalar_tensor_tensor(
-            out=minus_abs[:].rearrange("p j d -> p (j d)"),
-            in0=frac[:].rearrange("p j d -> p (j d)"),
-            scalar=-1.0,
-            in1=frac[:].rearrange("p j d -> p (j d)"),
-            op0=ALU.mult,
-            op1=ALU.min,
-        )
-        nc.scalar.activation(
-            out=cos_sin[:, :, 0:4:3, :],
-            in_=minus_abs[:].unsqueeze(2).to_broadcast(twice),
-            func=ACT.Sin,
-            scale=2.0 * math.pi,
-            bias=quarter_turn[:],
-        )
-        warm = const.tile([P, 1], F32)
-        nc.scalar.sqrt(out=warm[:], in_=one[:])
+        cos_sin = const.tile([P, J, 2, HALF], F32)
+
+        def make_angles(first_j, count):
+            js = slice(first_j, first_j + count)
+            shape = [P, count, HALF]
+            nc.vector.tensor_tensor(
+                out=turns[:, js, :],
+                in0=position[:, js].unsqueeze(2).to_broadcast(shape),
+                in1=per_position[:].unsqueeze(1).to_broadcast(shape),
+                op=ALU.mult,
+            )
+            nc.vector.tensor_scalar(
+                out=whole[:, js, :],
+                in0=turns[:, js, :],
+                scalar1=ROUND_MAGIC,
+                scalar2=ROUND_MAGIC,
+                op0=ALU.add,
+                op1=ALU.subtract,
+            )
+            nc.vector.tensor_tensor(out=frac[:, js, :], in0=turns[:, js, :], in1=whole[:, js, :], op=ALU.subtract)
+            nc.vector.scalar_tensor_tensor(
+                out=minus_abs[:, js, :].rearrange("p j d -> p (j d)"),
+                in0=frac[:, js, :].rearrange("p j d -> p (j d)"),
+                scalar=-1.0,
+                in1=frac[:, js, :].rearrange("p j d -> p (j d)"),
+                op0=ALU.mult,
+                op1=ALU.min,
+            )
+
+        def make_cos_sin(first_j, count):
+            js = slice(first_j, first_j + count)
+            nc.scalar.activation(out=cos_sin[:, js, 1, :], in_=frac[:, js, :], func=ACT.Sin, scale=2.0 * math.pi)
+            nc.scalar.activation(
+                out=cos_sin[:, js, 0, :],
+                in_=minus_abs[:, js, :],
+                func=ACT.Sin,
+                scale=2.0 * math.pi,
+                bias=quarter_turn[:],
+            )
+
+        make_angles(0, CHUNK)
+        make_cos_sin(0, CHUNK)
+        make_angles(CHUNK, J - CHUNK)
 
         gain = const.tile([P, 2, 2, 2, HALF], F32)
         gamma_halves = gamma_bf[:].rearrange("p a (h d) -> p a h d", h=2)
@@ -172,15 +190,23 @@ def tile_gqaattention_pa_t_kernel(
         nc.vector.tensor_scalar_mul(out=gain[:, :, 0, 1, :], in0=gamma_halves[:, :, 0, :], scalar1=-1.0)
         table = const.tile([P, J, 2, 2, 2, HALF], F32)
 
-        def fold_gains(row):
-            js = slice(CHUNK * row, CHUNK * (row + 1))
-            shape = [P, CHUNK, 2, 2 * HD]
-            nc.vector.tensor_tensor(
-                out=table[:, js].rearrange("p j a h r d -> p j a (h r d)"),
+        def fold_gains(engine, first_j, count):
+            js = slice(first_j, first_j + count)
+            shape = [P, count, 2, HD]
+            engine.tensor_tensor(
+                out=table[:, js, :, 0, :, :].rearrange("p j a h d -> p j a (h d)"),
                 in0=cos_sin[:, js].rearrange("p j r d -> p j (r d)").unsqueeze(2).to_broadcast(shape),
-                in1=gain[:].rearrange("p a h r d -> p a (h r d)").unsqueeze(1).to_broadcast(shape),
+                in1=gain[:, :, 0, :, :].rearrange("p a h d -> p a (h d)").unsqueeze(1).to_broadcast(shape),
                 op=ALU.mult,
             )
+            shape = [P, count, 2, HALF]
+            for half in range(2):
+                engine.tensor_tensor(
+                    out=table[:, js, :, 1, half, :],
+                    in0=cos_sin[:, js, 1 - half, :].unsqueeze(2).to_broadcast(shape),
+                    in1=gain[:, :, 1, half, :].unsqueeze(1).to_broadcast(shape),
+                    op=ALU.mult,
+                )
 
         xt_banks, x_codes, x_scales, grouped_tiles = {}, {}, {}, {}
         acc_banks, lengths, padded_lengths, inverse_norms = {}, {}, {}, {}
@@ -208,11 +234,11 @@ def tile_gqaattention_pa_t_kernel(
             x_codes[g] = quant.tile([P, PAIR, PASSES, P], U32, name="codes", align_bytes=64)
             x_scales[g] = quant.tile([P, PAIR, PASSES, P], U8, name="scales", align_bytes=64)
 
-        def quantise_tile(g, i):
+        def quantise_pair(g):
             nc.vector.quantize_mx(
-                out=x_codes[g][:, i].rearrange("p s t -> p (s t)").bitcast(FP8X4),
-                scales=x_scales[g][:, i].rearrange("p s t -> p (s t)"),
-                in_=grouped_tiles[g][:, i].rearrange("p s t e -> p (s t e)"),
+                out=x_codes[g][:].rearrange("p i s t -> p (i s t)").bitcast(FP8X4),
+                scales=x_scales[g][:].rearrange("p i s t -> p (i s t)"),
+                in_=grouped_tiles[g][:].rearrange("p i s t e -> p (i s t e)"),
             )
 
         def project_pair(g):
@@ -308,6 +334,9 @@ def tile_gqaattention_pa_t_kernel(
                 c = (g + TRANSPOSE_AHEAD) * PAIR // CHUNK
                 if (g + TRANSPOSE_AHEAD + 1) * PAIR % CHUNK == 0 and c + X_BUFS < CHUNKS:
                     load_chunk(c + X_BUFS)
+            if g + TRANSPOSE_AHEAD == 0:
+                make_cos_sin(CHUNK, J - CHUNK)
+                nc.scalar.sqrt(out=warm[:, 1:2], in_=one[:])
             if exists(g):
                 rope_products(g, 0)
             if exists(g + 1):
@@ -315,10 +344,9 @@ def tile_gqaattention_pa_t_kernel(
             if exists(g):
                 rope_products(g, 1)
             if exists(g + QUANTISE_AHEAD):
-                quantise_tile(g + QUANTISE_AHEAD, 0)
-                quantise_tile(g + QUANTISE_AHEAD, 1)
+                quantise_pair(g + QUANTISE_AHEAD)
             if g + TRANSPOSE_AHEAD < J // CHUNK:
-                fold_gains(g + TRANSPOSE_AHEAD)
+                fold_gains(nc.vector, CHUNK * (g + TRANSPOSE_AHEAD), CHUNK)
             if exists(g + PROJECT_AHEAD):
                 add_eps(g + PROJECT_AHEAD)
             if exists(g):

@@ -76,7 +76,7 @@ def tile_gqaattention_pa_t_kernel(
         def load_chunk(c):
             j0, b = CHUNK * (c // B), c % B
             x_sb = x_pool.tile([P, CHUNK, D], BF16, name="x_sb")
-            pieces = CHUNK // PAIR if c == 0 else 1
+            pieces = CHUNK if c == 0 else 1
             width = CHUNK // pieces
             for first_tile in range(0, CHUNK, width):
                 nc.sync.dma_start(
@@ -334,7 +334,7 @@ def tile_gqaattention_pa_t_kernel(
                 c = (g + TRANSPOSE_AHEAD) * PAIR // CHUNK
                 if (g + TRANSPOSE_AHEAD + 1) * PAIR % CHUNK == 0 and c + X_BUFS < CHUNKS:
                     load_chunk(c + X_BUFS)
-            if g + TRANSPOSE_AHEAD == 0:
+            if g + TRANSPOSE_AHEAD == 1:
                 make_cos_sin(CHUNK, J - CHUNK)
                 nc.scalar.sqrt(out=warm[:, 1:2], in_=one[:])
             if exists(g):

@@ -209,7 +209,7 @@ def tile_gqaattention_pa_t_kernel(
                 )
 
         xt_banks, x_codes, x_scales, grouped_tiles = {}, {}, {}, {}
-        acc_banks, lengths, padded_lengths, inverse_norms = {}, {}, {}, {}
+        acc_banks, sums_sq, lengths, padded_lengths, inverse_norms = {}, {}, {}, {}, {}
         v_tiles, out_tiles, term_tiles = {}, {}, {}
 
         def transpose_pair(g):
@@ -234,11 +234,12 @@ def tile_gqaattention_pa_t_kernel(
             x_codes[g] = quant.tile([P, PAIR, PASSES, P], U32, name="codes", align_bytes=64)
             x_scales[g] = quant.tile([P, PAIR, PASSES, P], U8, name="scales", align_bytes=64)
 
-        def quantise_pair(g):
+        def quantise(g, first, count):
+            tiles = slice(first, first + count)
             nc.vector.quantize_mx(
-                out=x_codes[g][:].rearrange("p i s t -> p (i s t)").bitcast(FP8X4),
-                scales=x_scales[g][:].rearrange("p i s t -> p (i s t)"),
-                in_=grouped_tiles[g][:].rearrange("p i s t e -> p (i s t e)"),
+                out=x_codes[g][:, tiles].rearrange("p i s t -> p (i s t)").bitcast(FP8X4),
+                scales=x_scales[g][:, tiles].rearrange("p i s t -> p (i s t)"),
+                in_=grouped_tiles[g][:, tiles].rearrange("p i s t e -> p (i s t e)"),
             )
 
         def project_pair(g):
@@ -260,7 +261,9 @@ def tile_gqaattention_pa_t_kernel(
         def norms_and_v(g):
             v_tiles[g] = results.tile([P, PAIR, HD], F32, name="v_sb")
             squares = norm.tile([P, PAIR * ROPED, HD], BF16, name="squares")
-            sum_sq = norm.tile([P, PAIR * ROPED], F32, name="sum_sq")
+            m, first = duo_of(g)
+            if m not in sums_sq:
+                sums_sq[m] = norm.tile([P, 2 * PAIR * ROPED], F32, name="sum_sq")
             for i in range(PAIR):
                 for h in range(ROPED):
                     col = ROPED * i + h
@@ -268,23 +271,29 @@ def tile_gqaattention_pa_t_kernel(
                         out=squares[:, col, :],
                         in_=acc_banks[g][i][:, HD * h : HD * (h + 1)],
                         func=ACT.Square,
-                        accum_out=sum_sq[:, col : col + 1],
+                        accum_out=sums_sq[m][:, first + col : first + col + 1],
                     )
             for i in range(PAIR):
                 nc.scalar.copy(out=v_tiles[g][:, i, :], in_=acc_banks[g][i][:, HD * ROPED :])
-            length = norm.tile([P, PAIR * ROPED], F32, name="length")
-            nc.scalar.sqrt(out=length[:], in_=sum_sq[:])
-            lengths[g] = length
+            if first > 0 or g == PAIRS - 1:
+                lengths[m] = norm.tile([P, 2 * PAIR * ROPED], F32, name="length")
+                nc.scalar.sqrt(out=lengths[m][:, columns_of(m)], in_=sums_sq[m][:, columns_of(m)])
 
-        def add_eps(g):
-            padded = norm.tile([P, PAIR * ROPED], F32, name="padded")
-            nc.vector.tensor_scalar_add(out=padded[:], in0=lengths[g][:], scalar1=EPS)
-            padded_lengths[g] = padded
+        def duo_of(g):
+            return (g + 1) // 2, PAIR * ROPED * ((g + 1) % 2)
 
-        def invert(g):
-            inverse = norm.tile([P, PAIR * ROPED], F32, name="inverse")
-            nc.vector.reciprocal(out=inverse[:], in_=padded_lengths[g][:])
-            inverse_norms[g] = inverse
+        def columns_of(m):
+            return slice(PAIR * ROPED if m == 0 else 0, PAIR * ROPED if 2 * m == PAIRS else 2 * PAIR * ROPED)
+
+        def add_eps(m):
+            padded_lengths[m] = norm.tile([P, 2 * PAIR * ROPED], F32, name="padded")
+            nc.vector.tensor_scalar_add(
+                out=padded_lengths[m][:, columns_of(m)], in0=lengths[m][:, columns_of(m)], scalar1=EPS
+            )
+
+        def invert(m):
+            inverse_norms[m] = norm.tile([P, 2 * PAIR * ROPED], F32, name="inverse")
+            nc.vector.reciprocal(out=inverse_norms[m][:, columns_of(m)], in_=padded_lengths[m][:, columns_of(m)])
 
         def rope_products(g, i):
             j = CHUNK * (g * PAIR // CHUNK // B) + g * PAIR % CHUNK + i
@@ -295,7 +304,7 @@ def tile_gqaattention_pa_t_kernel(
                 nc.vector.scalar_tensor_tensor(
                     out=term_tiles[g][:, h, i, :, :, :].rearrange("p r a d -> p r (a d)"),
                     in0=acc_banks[g][i][:, HD * h : HD * (h + 1)].unsqueeze(1).to_broadcast([P, 2, HD]),
-                    scalar=inverse_norms[g][:, ROPED * i + h : ROPED * i + h + 1],
+                    scalar=inverse_norms[duo_of(g)[0]][:, duo_of(g)[1] + ROPED * i + h : duo_of(g)[1] + ROPED * i + h + 1],
                     in1=table[:, j, which, :, :, :].rearrange("p r a d -> p r (a d)"),
                     op0=ALU.mult,
                     op1=ALU.mult,
@@ -339,16 +348,19 @@ def tile_gqaattention_pa_t_kernel(
                 nc.scalar.sqrt(out=warm[:, 1:2], in_=one[:])
             if exists(g):
                 rope_products(g, 0)
-            if exists(g + 1):
-                invert(g + 1)
-            if exists(g):
                 rope_products(g, 1)
-            if exists(g + QUANTISE_AHEAD):
-                quantise_pair(g + QUANTISE_AHEAD)
+            if g % 2 == 0 and (exists(g + 1) or exists(g + 2)):
+                m = duo_of(g + 2)[0]
+                add_eps(m)
+                if exists(g + QUANTISE_AHEAD):
+                    quantise(g + QUANTISE_AHEAD, 0, 1)
+                invert(m)
+                if exists(g + QUANTISE_AHEAD):
+                    quantise(g + QUANTISE_AHEAD, 1, 1)
+            elif exists(g + QUANTISE_AHEAD):
+                quantise(g + QUANTISE_AHEAD, 0, PAIR)
             if g + TRANSPOSE_AHEAD < J // CHUNK:
                 fold_gains(nc.vector, CHUNK * (g + TRANSPOSE_AHEAD), CHUNK)
-            if exists(g + PROJECT_AHEAD):
-                add_eps(g + PROJECT_AHEAD)
             if exists(g):
                 add_terms(g)
                 store_pair(g)

@@ -59,10 +59,10 @@ def tile_gqaattention_pa_t_kernel(
         ctx.enter_context(tc.manual_schedule())
         const = ctx.enter_context(tc.tile_pool(name="const", bufs=1))
         x_pool = ctx.enter_context(tc.tile_pool(name="x", bufs=X_BUFS))
-        quant = ctx.enter_context(tc.tile_pool(name="quant", bufs=4))
-        norm = ctx.enter_context(tc.tile_pool(name="norm", bufs=4))
-        terms = ctx.enter_context(tc.tile_pool(name="terms", bufs=3))
-        results = ctx.enter_context(tc.tile_pool(name="results", bufs=6))
+        quant = ctx.enter_context(tc.tile_pool(name="quant", bufs=5))
+        norm = ctx.enter_context(tc.tile_pool(name="norm", bufs=6))
+        terms = ctx.enter_context(tc.tile_pool(name="terms", bufs=5))
+        results = ctx.enter_context(tc.tile_pool(name="results", bufs=8))
         psum_xt = ctx.enter_context(tc.psum_pool(name="psum_xt", bufs=PAIR))
         psum_acc = ctx.enter_context(tc.psum_pool(name="psum_acc", bufs=(PROJECT_AHEAD + 1) * PAIR))
 

@@ -36,6 +36,7 @@ QUANTISE_AHEAD = 4
 TRANSPOSE_AHEAD = 5
 ROUND_MAGIC = 1.5 * 2.0**23
 
+QT, NT, AT = 2, 4, 2
 FLOPS = 2 * B * T * D * N_ALL
 
 
@@ -76,7 +77,7 @@ def tile_gqaattention_pa_t_kernel(
         def load_chunk(c):
             j0, b = CHUNK * (c // B), c % B
             x_sb = x_pool.tile([P, CHUNK, D], BF16, name="x_sb")
-            pieces = CHUNK if c == 0 else 1
+            pieces = 2 if c == 0 else 1
             width = CHUNK // pieces
             for first_tile in range(0, CHUNK, width):
                 nc.sync.dma_start(
@@ -85,109 +86,93 @@ def tile_gqaattention_pa_t_kernel(
                 )
             x_tiles[c] = x_sb
 
-        load_chunk(0)
-        gamma_bf = const.tile([P, 2, HD], BF16)
-        nc.sync.dma_start(out=gamma_bf[:, 0, :], in_=gamma_q.partition_broadcast(P))
-        nc.sync.dma_start(out=gamma_bf[:, 1, :], in_=gamma_k.partition_broadcast(P))
 
-        w_words = const.tile([P, PASSES, N_ALL], U32, align_bytes=64)
-        w_scales = const.tile([P, PASSES, N_ALL], U8, align_bytes=64)
-        nc.vector.memset(w_scales[:].bitcast(I32), 0)
+        gamma_rows = const.tile([P, 2, HD], BF16)
+        signs = const.tile([P, 2, P], BF16)
         one = const.tile([P, 1], F32)
+        nc.vector.memset(gamma_rows[:], 0.0)
         nc.vector.memset(one[:], 1.0)
         warm = const.tile([P, 2], F32)
         nc.scalar.activation(out=warm[:, 0:1], in_=one[:], func=ACT.Sin)
-        first = 0
-        for words, scales in ((wq_words, wq_scales), (wk_words, wk_scales), (wv_words, wv_scales)):
-            cols = slice(first, first + words.shape[2])
-            first += words.shape[2]
-            for quadrant in range(4):
-                nc.sync.dma_start(
-                    out=w_scales[32 * quadrant : 32 * quadrant + 4, :, cols].bitcast(I32),
-                    in_=scales[:, 4 * quadrant : 4 * quadrant + 4, :]
-                    .rearrange("g r n -> r g n")
-                    .bitcast(I32),
-                )
-            nc.sync.dma_start(
-                out=w_words[:, :, cols].bitcast(I32),
-                in_=words.rearrange("g p n t -> p g (n t)").bitcast(I32),
-            )
-
-        for c in range(1, X_BUFS):
-            load_chunk(c)
-
         position_i = const.tile([P, J], I32)
         nc.gpsimd.iota(position_i[:], pattern=[[1, J]], base=0, channel_multiplier=J)
         ident = const.tile([P, P], F32)
         make_identity(nc, ident[:])
-
+        w_words = const.tile([P, PASSES, N_ALL], U32, align_bytes=64)
+        w_scales = const.tile([P, PASSES, N_ALL], U8, align_bytes=64)
+        nc.sync.dma_start(out=gamma_rows[0:1, 0, :], in_=gamma_q.unsqueeze(0))
+        nc.sync.dma_start(out=gamma_rows[0:1, 1, :], in_=gamma_k.unsqueeze(0))
+        load_chunk(0)
+        groups = ((wq_words, wq_scales), (wk_words, wk_scales), (wv_words, wv_scales))
+        def load_words():
+            first = 0
+            for words, scales in groups:
+                cols = slice(first, first + words.shape[2])
+                first += words.shape[2]
+                nc.sync.dma_start(out=w_words[:, :, cols].bitcast(I32), in_=words.rearrange("g p n t -> p g (n t)").bitcast(I32))
+        def load_scales():
+            first = 0
+            for words, scales in groups:
+                cols = slice(first, first + words.shape[2])
+                first += words.shape[2]
+                for quadrant in range(4):
+                    nc.sync.dma_start(
+                        out=w_scales[32 * quadrant : 32 * quadrant + 4, :, cols].bitcast(I32),
+                        in_=scales[:, 4 * quadrant : 4 * quadrant + 4, :].rearrange("g r n -> r g n").bitcast(I32))
         quarter_turn = const.tile([P, 1], F32)
-        nc.vector.tensor_scalar_mul(out=quarter_turn[:], in0=one[:], scalar1=math.pi / 2)
         position = const.tile([P, J], F32)
-        nc.vector.tensor_copy(out=position[:], in_=position_i[:])
         per_position = const.tile([P, HALF], F32)
         nc.vector.tensor_scalar_mul(out=per_position[:, 0:1], in0=one[:], scalar1=1.0 / (2.0 * math.pi))
+        nc.vector.memset(signs[:, 0, :], 1.0)
+        nc.vector.memset(signs[:, 1, :], -1.0)
+        nc.vector.memset(w_scales[:].bitcast(I32), 0)
         width = 1
         while width < HALF:
-            nc.vector.tensor_scalar_mul(
-                out=per_position[:, width : 2 * width],
-                in0=per_position[:, 0:width],
-                scalar1=ROPE_BASE ** (-width / HALF),
-            )
-            width *= 2
+            for copy in range(1, 4):
+                nc.vector.tensor_scalar_mul(
+                    out=per_position[:, copy * width : (copy + 1) * width],
+                    in0=per_position[:, 0:width],
+                    scalar1=ROPE_BASE ** (-copy * width / HALF),
+                )
+            width *= 4
+            if width == 4:
+                nc.vector.tensor_copy(out=position[:, 0:CHUNK], in_=position_i[:, 0:CHUNK])
+            if width == 16:
+                nc.vector.tensor_scalar_mul(out=quarter_turn[:], in0=one[:], scalar1=math.pi / 2)
+        load_words()
+        load_chunk(1)
+        load_scales()
+        for c in range(2, X_BUFS):
+            load_chunk(c)
         turns = const.tile([P, J, HALF], F32)
         whole = const.tile([P, J, HALF], F32)
         frac = const.tile([P, J, HALF], F32)
-        minus_abs = const.tile([P, J, HALF], F32)
+        absolute = const.tile([P, J, HALF], F32)
         cos_sin = const.tile([P, J, 2, HALF], F32)
 
-        def make_angles(first_j, count):
+        def make_angles(engine, first_j, count):
             js = slice(first_j, first_j + count)
             shape = [P, count, HALF]
-            nc.vector.tensor_tensor(
-                out=turns[:, js, :],
-                in0=position[:, js].unsqueeze(2).to_broadcast(shape),
-                in1=per_position[:].unsqueeze(1).to_broadcast(shape),
-                op=ALU.mult,
-            )
-            nc.vector.tensor_scalar(
-                out=whole[:, js, :],
-                in0=turns[:, js, :],
-                scalar1=ROUND_MAGIC,
-                scalar2=ROUND_MAGIC,
-                op0=ALU.add,
-                op1=ALU.subtract,
-            )
-            nc.vector.tensor_tensor(out=frac[:, js, :], in0=turns[:, js, :], in1=whole[:, js, :], op=ALU.subtract)
-            nc.vector.scalar_tensor_tensor(
-                out=minus_abs[:, js, :].rearrange("p j d -> p (j d)"),
-                in0=frac[:, js, :].rearrange("p j d -> p (j d)"),
-                scalar=-1.0,
-                in1=frac[:, js, :].rearrange("p j d -> p (j d)"),
-                op0=ALU.mult,
-                op1=ALU.min,
-            )
+            engine.tensor_tensor(out=turns[:, js, :], in0=position[:, js].unsqueeze(2).to_broadcast(shape), in1=per_position[:].unsqueeze(1).to_broadcast(shape), op=ALU.mult)
+            engine.tensor_scalar(out=whole[:, js, :], in0=turns[:, js, :], scalar1=ROUND_MAGIC, scalar2=ROUND_MAGIC, op0=ALU.add, op1=ALU.subtract)
+            engine.tensor_tensor(out=frac[:, js, :], in0=turns[:, js, :], in1=whole[:, js, :], op=ALU.subtract)
 
         def make_cos_sin(first_j, count):
             js = slice(first_j, first_j + count)
+            nc.scalar.activation(out=absolute[:, js, :], in_=frac[:, js, :], func=ACT.Abs)
             nc.scalar.activation(out=cos_sin[:, js, 1, :], in_=frac[:, js, :], func=ACT.Sin, scale=2.0 * math.pi)
-            nc.scalar.activation(
-                out=cos_sin[:, js, 0, :],
-                in_=minus_abs[:, js, :],
-                func=ACT.Sin,
-                scale=2.0 * math.pi,
-                bias=quarter_turn[:],
-            )
+            nc.scalar.activation(out=cos_sin[:, js, 0, :], in_=absolute[:, js, :], func=ACT.Sin, scale=-2.0 * math.pi, bias=quarter_turn[:])
 
-        make_angles(0, CHUNK)
+        make_angles(nc.vector, 0, CHUNK)
+        nc.vector.tensor_copy(out=position[:, CHUNK:], in_=position_i[:, CHUNK:])
         make_cos_sin(0, CHUNK)
-        make_angles(CHUNK, J - CHUNK)
-
-        gain = const.tile([P, 2, 2, 2, HALF], F32)
-        gamma_halves = gamma_bf[:].rearrange("p a (h d) -> p a h d", h=2)
-        nc.vector.tensor_copy(out=gain[:, :, :, 0, :], in_=gamma_halves)
-        nc.vector.tensor_copy(out=gain[:, :, 1, 1, :], in_=gamma_halves[:, :, 1, :])
-        nc.vector.tensor_scalar_mul(out=gain[:, :, 0, 1, :], in0=gamma_halves[:, :, 0, :], scalar1=-1.0)
+        gain = psum_acc.tile([P, 2, 2, 2, HALF], F32, name="acc")
+        halves = gamma_rows[:].rearrange("p a (h d) -> p a h d", h=2)
+        for hu in range(2):
+            nc.tensor.matmul(out=gain[:, :, :, hu, :], lhsT=signs[:, 0, :], rhs=halves, start=True, stop=True)
+        nc.tensor.matmul(out=gain[:, :, 0, 1, :], lhsT=signs[:, 1, :], rhs=halves[:, :, 0, :], start=True, stop=True)
+        for first_j in range(CHUNK, J, CHUNK):
+            make_angles(nc.vector, first_j, CHUNK)
         table = const.tile([P, J, 2, 2, 2, HALF], F32)
 
         def fold_gains(engine, first_j, count):
@@ -196,171 +181,150 @@ def tile_gqaattention_pa_t_kernel(
             engine.tensor_tensor(
                 out=table[:, js, :, 0, :, :].rearrange("p j a h d -> p j a (h d)"),
                 in0=cos_sin[:, js].rearrange("p j r d -> p j (r d)").unsqueeze(2).to_broadcast(shape),
-                in1=gain[:, :, 0, :, :].rearrange("p a h d -> p a (h d)").unsqueeze(1).to_broadcast(shape),
-                op=ALU.mult,
-            )
+                in1=gain[:, :, 0, :, :].rearrange("p a h d -> p a (h d)").unsqueeze(1).to_broadcast(shape), op=ALU.mult)
             shape = [P, count, 2, HALF]
             for half in range(2):
                 engine.tensor_tensor(
                     out=table[:, js, :, 1, half, :],
                     in0=cos_sin[:, js, 1 - half, :].unsqueeze(2).to_broadcast(shape),
-                    in1=gain[:, :, 1, half, :].unsqueeze(1).to_broadcast(shape),
-                    op=ALU.mult,
-                )
+                    in1=gain[:, :, 1, half, :].unsqueeze(1).to_broadcast(shape), op=ALU.mult)
 
         xt_banks, x_codes, x_scales, grouped_tiles = {}, {}, {}, {}
-        acc_banks, sums_sq, lengths, padded_lengths, inverse_norms = {}, {}, {}, {}, {}
+        acc_banks, sums_sq, lengths, padded, inverse = {}, {}, {}, {}, {}
         v_tiles, out_tiles, term_tiles = {}, {}, {}
+        TILES = B * J
 
-        def transpose_pair(g):
-            c, first_tile = g * PAIR // CHUNK, g * PAIR % CHUNK
+        def place(t):
+            c = t // CHUNK
+            return c, t % CHUNK, c % B, CHUNK * (c // B) + t % CHUNK
+
+        def transpose(t):
+            c, i, b, j = place(t)
             words = x_tiles[c][:].bitcast(F32).rearrange("p j (s w u) -> p j s u w", s=PASSES, u=2)
-            xt_banks[g] = []
-            for i in range(PAIR):
-                xt = psum_xt.tile([P, PASSES, 2, P], F32, name="xt")
-                for s in range(PASSES):
-                    for u in range(2):
-                        nc.tensor.transpose(xt[:, s, u, :], words[:, first_tile + i, s, u, :], ident[:])
-                xt_banks[g].append(xt)
+            xt = psum_xt.tile([P, PASSES, 2, P], F32, name="xt")
+            for s in range(PASSES):
+                for u in range(2):
+                    nc.tensor.transpose(xt[:, s, u, :], words[:, i, s, u, :], ident[:])
+            xt_banks[t] = xt
 
-        def regroup_pair(g):
-            grouped = quant.tile([P, PAIR, PASSES, P, 4], BF16, name="grouped", align_bytes=64)
-            for i in range(PAIR):
-                nc.scalar.copy(
-                    out=grouped[:, i].bitcast(F32),
-                    in_=xt_banks[g][i][:].rearrange("p s u t -> p s t u"),
-                )
-            grouped_tiles[g] = grouped
-            x_codes[g] = quant.tile([P, PAIR, PASSES, P], U32, name="codes", align_bytes=64)
-            x_scales[g] = quant.tile([P, PAIR, PASSES, P], U8, name="scales", align_bytes=64)
+        def regroup(t):
+            q = t // QT
+            if t % QT == 0:
+                grouped_tiles[q] = quant.tile([P, QT, PASSES, P, 4], BF16, name="grouped", align_bytes=64)
+                x_codes[q] = quant.tile([P, QT, PASSES, P], U32, name="codes", align_bytes=64)
+                x_scales[q] = quant.tile([P, QT, PASSES, P], U8, name="scales", align_bytes=64)
+            nc.scalar.copy(out=grouped_tiles[q][:, t % QT].bitcast(F32), in_=xt_banks[t][:].rearrange("p s u t -> p s t u"))
 
-        def quantise(g, first, count):
-            tiles = slice(first, first + count)
+        def quantise(t, count):
+            q = t // QT
+            tiles = slice(t % QT, t % QT + count)
             nc.vector.quantize_mx(
-                out=x_codes[g][:, tiles].rearrange("p i s t -> p (i s t)").bitcast(FP8X4),
-                scales=x_scales[g][:, tiles].rearrange("p i s t -> p (i s t)"),
-                in_=grouped_tiles[g][:, tiles].rearrange("p i s t e -> p (i s t e)"),
+                out=x_codes[q][:, tiles].rearrange("p i s t -> p (i s t)").bitcast(FP8X4),
+                scales=x_scales[q][:, tiles].rearrange("p i s t -> p (i s t)"),
+                in_=grouped_tiles[q][:, tiles].rearrange("p i s t e -> p (i s t e)"),
             )
 
-        def project_pair(g):
-            acc_banks[g] = []
-            for i in range(PAIR):
-                acc = psum_acc.tile([P, N_ALL], F32, name="acc")
-                for s in range(PASSES):
-                    nc.tensor.matmul_mx(
-                        out=acc[:],
-                        lhsT=x_codes[g][:, i, s, :].bitcast(FP8X4),
-                        lhsT_scale=x_scales[g][:, i, s, :],
-                        rhs=w_words[:, s, :].bitcast(FP8X4),
-                        rhs_scale=w_scales[:, s, :],
-                        start=(s == 0),
-                        stop=(s == PASSES - 1),
-                    )
-                acc_banks[g].append(acc)
+        def project(t):
+            q, i = t // QT, t % QT
+            acc = psum_acc.tile([P, N_ALL], F32, name="acc")
+            for s in range(PASSES):
+                nc.tensor.matmul_mx(
+                    out=acc[:], lhsT=x_codes[q][:, i, s, :].bitcast(FP8X4), lhsT_scale=x_scales[q][:, i, s, :],
+                    rhs=w_words[:, s, :].bitcast(FP8X4), rhs_scale=w_scales[:, s, :], start=(s == 0), stop=(s == PASSES - 1))
+            acc_banks[t] = acc
 
-        def norms_and_v(g):
-            v_tiles[g] = results.tile([P, PAIR, HD], F32, name="v_sb")
-            squares = norm.tile([P, PAIR * ROPED, HD], BF16, name="squares")
-            m, first = duo_of(g)
-            if m not in sums_sq:
-                sums_sq[m] = norm.tile([P, 2 * PAIR * ROPED], F32, name="sum_sq")
-            for i in range(PAIR):
-                for h in range(ROPED):
-                    col = ROPED * i + h
-                    nc.scalar.activation(
-                        out=squares[:, col, :],
-                        in_=acc_banks[g][i][:, HD * h : HD * (h + 1)],
-                        func=ACT.Square,
-                        accum_out=sums_sq[m][:, first + col : first + col + 1],
-                    )
-            for i in range(PAIR):
-                nc.scalar.copy(out=v_tiles[g][:, i, :], in_=acc_banks[g][i][:, HD * ROPED :])
-            if first > 0 or g == PAIRS - 1:
-                lengths[m] = norm.tile([P, 2 * PAIR * ROPED], F32, name="length")
-                nc.scalar.sqrt(out=lengths[m][:, columns_of(m)], in_=sums_sq[m][:, columns_of(m)])
+        def squares(t):
+            n = (t + 2) // NT
+            if n not in sums_sq:
+                sums_sq[n] = norm.tile([P, NT * ROPED], F32, name="sum_sq")
+            junk = norm.tile([P, ROPED, HD], BF16, name="squares")
+            for h in range(ROPED):
+                col = ROPED * ((t + 2) % NT) + h
+                nc.scalar.activation(out=junk[:, h, :], in_=acc_banks[t][:, HD * h : HD * (h + 1)], func=ACT.Square, accum_out=sums_sq[n][:, col : col + 1])
 
-        def duo_of(g):
-            return (g + 1) // 2, PAIR * ROPED * ((g + 1) % 2)
+        def copy_v(t):
+            m = t // AT
+            if t % AT == 0:
+                v_tiles[m] = results.tile([P, AT, HD], F32, name="v_sb")
+            nc.scalar.copy(out=v_tiles[m][:, t % AT, :], in_=acc_banks[t][:, HD * ROPED :])
 
-        def columns_of(m):
-            return slice(PAIR * ROPED if m == 0 else 0, PAIR * ROPED if 2 * m == PAIRS else 2 * PAIR * ROPED)
+        def span(n): return slice(2 * ROPED if n == 0 else 0, 2 * ROPED if n == TILES // 4 else 4 * ROPED)
 
-        def add_eps(m):
-            padded_lengths[m] = norm.tile([P, 2 * PAIR * ROPED], F32, name="padded")
-            nc.vector.tensor_scalar_add(
-                out=padded_lengths[m][:, columns_of(m)], in0=lengths[m][:, columns_of(m)], scalar1=EPS
-            )
+        def root(n):
+            lengths[n] = norm.tile([P, NT * ROPED], F32, name="length")
+            nc.scalar.sqrt(out=lengths[n][:, span(n)], in_=sums_sq[n][:, span(n)])
 
-        def invert(m):
-            inverse_norms[m] = norm.tile([P, 2 * PAIR * ROPED], F32, name="inverse")
-            nc.vector.reciprocal(out=inverse_norms[m][:, columns_of(m)], in_=padded_lengths[m][:, columns_of(m)])
+        def add_eps(n, engine=None):
+            padded[n] = norm.tile([P, NT * ROPED], F32, name="padded")
+            if engine is None: nc.vector.tensor_scalar_add(out=padded[n][:, span(n)], in0=lengths[n][:, span(n)], scalar1=EPS)
+            else: nc.scalar.add(padded[n][:, span(n)], lengths[n][:, span(n)], EPS)
 
-        def rope_products(g, i):
-            j = CHUNK * (g * PAIR // CHUNK // B) + g * PAIR % CHUNK + i
-            if i == 0:
-                term_tiles[g] = terms.tile([P, ROPED, PAIR, 2, 2, HALF], F32, name="terms")
+        def invert(n):
+            inverse[n] = norm.tile([P, NT * ROPED], F32, name="inverse")
+            nc.vector.reciprocal(out=inverse[n][:, span(n)], in_=padded[n][:, span(n)])
+
+        def rope(t):
+            c, i, b, j = place(t)
+            m, n = t // AT, (t + 2) // NT
+            if t % AT == 0:
+                term_tiles[m] = terms.tile([P, ROPED, AT, 2, 2, HALF], F32, name="terms")
             for h in range(ROPED):
                 which = 0 if h < Q_HEADS else 1
+                col = ROPED * ((t + 2) % NT) + h
                 nc.vector.scalar_tensor_tensor(
-                    out=term_tiles[g][:, h, i, :, :, :].rearrange("p r a d -> p r (a d)"),
-                    in0=acc_banks[g][i][:, HD * h : HD * (h + 1)].unsqueeze(1).to_broadcast([P, 2, HD]),
-                    scalar=inverse_norms[duo_of(g)[0]][:, duo_of(g)[1] + ROPED * i + h : duo_of(g)[1] + ROPED * i + h + 1],
+                    out=term_tiles[m][:, h, t % AT, :, :, :].rearrange("p r a d -> p r (a d)"),
+                    in0=acc_banks[t][:, HD * h : HD * (h + 1)].unsqueeze(1).to_broadcast([P, 2, HD]),
+                    scalar=inverse[n][:, col : col + 1],
                     in1=table[:, j, which, :, :, :].rearrange("p r a d -> p r (a d)"),
-                    op0=ALU.mult,
-                    op1=ALU.mult,
-                )
+                    op0=ALU.mult, op1=ALU.mult)
 
-        def add_terms(g):
-            out_tiles[g] = results.tile([P, ROPED, PAIR, 2, HALF], F32, name="qk_sb")
-            engine = nc.gpsimd if g < PAIRS - 1 else nc.vector
-            engine.tensor_tensor(
-                out=out_tiles[g][:],
-                in0=term_tiles[g][:, :, :, :, 0, :],
-                in1=term_tiles[g][:, :, :, :, 1, :],
-                op=ALU.add,
-            )
+        def add_terms(m, engine=None, first=0, count=None):
+            count = count or AT
+            if first == 0:
+                out_tiles[m] = results.tile([P, ROPED, AT, 2, HALF], F32, name="qk_sb")
+            sl = slice(first, first + count)
+            (engine or nc.gpsimd).tensor_tensor(out=out_tiles[m][:, :, sl], in0=term_tiles[m][:, :, sl, :, 0, :], in1=term_tiles[m][:, :, sl, :, 1, :], op=ALU.add)
 
-        def store_pair(g):
-            c, first_tile = g * PAIR // CHUNK, g * PAIR % CHUNK
-            b = c % B
-            js = slice(CHUNK * (c // B) + first_tile, CHUNK * (c // B) + first_tile + PAIR)
-            nc.sync.dma_start(out=v_view[b, :, 0, js, :], in_=v_tiles[g][:])
-            qk = out_tiles[g][:].rearrange("p h i a d -> p h i (a d)")
-            nc.sync.dma_start(out=q_view[b, :, :, js, :], in_=qk[:, 0:Q_HEADS, :, :])
-            nc.sync.dma_start(out=k_view[b, :, 0, js, :], in_=qk[:, Q_HEADS, :, :])
+        def store(m, first=0, count=None):
+            count = count or AT
+            c, i, b, j = place(m * AT + first)
+            js = slice(j, j + count)
+            sl = slice(first, first + count)
+            qk = out_tiles[m][:].rearrange("p h i a d -> p h i (a d)")
+            nc.sync.dma_start(out=q_view[b, :, :, js, :], in_=qk[:, 0:Q_HEADS, sl, :])
+            nc.sync.dma_start(out=k_view[b, :, 0, js, :], in_=qk[:, Q_HEADS, sl, :])
 
-
-        def exists(pair):
-            return 0 <= pair < PAIRS
+        def store_v(m):
+            c, i, b, j = place(m * AT)
+            nc.sync.dma_start(out=v_view[b, :, 0, slice(j, j + AT), :], in_=v_tiles[m][:])
+        def ok(t): return 0 <= t < TILES
 
         for g in range(-TRANSPOSE_AHEAD, PAIRS):
-            if exists(g + PROJECT_AHEAD):
-                project_pair(g + PROJECT_AHEAD)
-                norms_and_v(g + PROJECT_AHEAD)
-            if exists(g + TRANSPOSE_AHEAD):
-                transpose_pair(g + TRANSPOSE_AHEAD)
-                regroup_pair(g + TRANSPOSE_AHEAD)
-                c = (g + TRANSPOSE_AHEAD) * PAIR // CHUNK
-                if (g + TRANSPOSE_AHEAD + 1) * PAIR % CHUNK == 0 and c + X_BUFS < CHUNKS:
-                    load_chunk(c + X_BUFS)
-            if g + TRANSPOSE_AHEAD == 1:
-                make_cos_sin(CHUNK, J - CHUNK)
+            p, r = 2 * (g + PROJECT_AHEAD), 2 * (g + TRANSPOSE_AHEAD)
+            if ok(p):
+                project(p); project(p + 1)
+                squares(p); squares(p + 1); copy_v(p); copy_v(p + 1)
+                if (p // 2) % 2 == 0 or p == 2 * PAIRS - 2: root((p + 2) // 4)
+            if ok(r):
+                transpose(r); transpose(r + 1); regroup(r); regroup(r + 1)
+                c = r // CHUNK
+                if (r + 2) % CHUNK == 0 and c + X_BUFS < CHUNKS: load_chunk(c + X_BUFS)
+            if r == 0: make_cos_sin(CHUNK, CHUNK)
+            if r == 2: make_cos_sin(2 * CHUNK, CHUNK)
+            if r == 4:
+                make_cos_sin(3 * CHUNK, CHUNK)
                 nc.scalar.sqrt(out=warm[:, 1:2], in_=one[:])
-            if exists(g):
-                rope_products(g, 0)
-                rope_products(g, 1)
-            if g % 2 == 0 and (exists(g + 1) or exists(g + 2)):
-                m = duo_of(g + 2)[0]
-                add_eps(m)
-                if exists(g + QUANTISE_AHEAD):
-                    quantise(g + QUANTISE_AHEAD, 0, 1)
-                invert(m)
-                if exists(g + QUANTISE_AHEAD):
-                    quantise(g + QUANTISE_AHEAD, 1, 1)
-            elif exists(g + QUANTISE_AHEAD):
-                quantise(g + QUANTISE_AHEAD, 0, PAIR)
-            if g + TRANSPOSE_AHEAD < J // CHUNK:
-                fold_gains(nc.vector, CHUNK * (g + TRANSPOSE_AHEAD), CHUNK)
-            if exists(g):
-                add_terms(g)
-                store_pair(g)
+            t = 2 * g
+            if ok(t): rope(t); rope(t + 1)
+            q = 2 * (g + QUANTISE_AHEAD)
+            if g % 2 == 0 and (ok(t + 2) or ok(t + 4)):
+                n = (t + 4 + 2) // 4
+                add_eps(n)
+                if ok(q): quantise(q, 1)
+                invert(n)
+                if ok(q): quantise(q + 1, 1)
+            elif ok(q): quantise(q, 2)
+            if g + TRANSPOSE_AHEAD < J // CHUNK: fold_gains(nc.vector, CHUNK * (g + TRANSPOSE_AHEAD), CHUNK)
+            if ok(t):
+                add_terms(g, nc.gpsimd if g < PAIRS - 1 else nc.vector)
+                store_v(g); store(g)

@@ -77,7 +77,7 @@ def tile_gqaattention_pa_t_kernel(
         def load_chunk(c):
             j0, b = CHUNK * (c // B), c % B
             x_sb = x_pool.tile([P, CHUNK, D], BF16, name="x_sb")
-            pieces = 2 if c == 0 else 1
+            pieces = 4 if c == 0 else 1
             width = CHUNK // pieces
             for first_tile in range(0, CHUNK, width):
                 nc.sync.dma_start(
@@ -139,13 +139,13 @@ def tile_gqaattention_pa_t_kernel(
                 nc.vector.tensor_copy(out=position[:, 0:CHUNK], in_=position_i[:, 0:CHUNK])
             if width == 16:
                 nc.vector.tensor_scalar_mul(out=quarter_turn[:], in0=one[:], scalar1=math.pi / 2)
-        load_words()
         load_chunk(1)
+        load_words()
         load_scales()
         for c in range(2, X_BUFS):
             load_chunk(c)
-        turns = const.tile([P, J, HALF], F32)
-        whole = const.tile([P, J, HALF], F32)
+        WRAP = sum(1 for d in range(HALF) if (T - 1) * ROPE_BASE ** (-d / HALF) > math.pi)
+        whole = const.tile([P, J, WRAP], F32)
         frac = const.tile([P, J, HALF], F32)
         absolute = const.tile([P, J, HALF], F32)
         cos_sin = const.tile([P, J, 2, HALF], F32)
@@ -153,17 +153,26 @@ def tile_gqaattention_pa_t_kernel(
         def make_angles(engine, first_j, count):
             js = slice(first_j, first_j + count)
             shape = [P, count, HALF]
-            engine.tensor_tensor(out=turns[:, js, :], in0=position[:, js].unsqueeze(2).to_broadcast(shape), in1=per_position[:].unsqueeze(1).to_broadcast(shape), op=ALU.mult)
-            engine.tensor_scalar(out=whole[:, js, :], in0=turns[:, js, :], scalar1=ROUND_MAGIC, scalar2=ROUND_MAGIC, op0=ALU.add, op1=ALU.subtract)
-            engine.tensor_tensor(out=frac[:, js, :], in0=turns[:, js, :], in1=whole[:, js, :], op=ALU.subtract)
+            engine.tensor_tensor(out=frac[:, js, :], in0=position[:, js].unsqueeze(2).to_broadcast(shape), in1=per_position[:].unsqueeze(1).to_broadcast(shape), op=ALU.mult)
+            engine.tensor_scalar(out=whole[:, js, :], in0=frac[:, js, 0:WRAP], scalar1=ROUND_MAGIC, scalar2=ROUND_MAGIC, op0=ALU.add, op1=ALU.subtract)
+            engine.tensor_tensor(out=frac[:, js, 0:WRAP], in0=frac[:, js, 0:WRAP], in1=whole[:, js, :], op=ALU.subtract)
 
         def make_cos_sin(first_j, count):
             js = slice(first_j, first_j + count)
-            nc.scalar.activation(out=absolute[:, js, :], in_=frac[:, js, :], func=ACT.Abs)
+            if first_j:
+                nc.scalar.activation(out=absolute[:, js, :], in_=frac[:, js, :], func=ACT.Abs)
             nc.scalar.activation(out=cos_sin[:, js, 1, :], in_=frac[:, js, :], func=ACT.Sin, scale=2.0 * math.pi)
             nc.scalar.activation(out=cos_sin[:, js, 0, :], in_=absolute[:, js, :], func=ACT.Sin, scale=-2.0 * math.pi, bias=quarter_turn[:])
 
         make_angles(nc.vector, 0, CHUNK)
+        nc.vector.scalar_tensor_tensor(
+            out=absolute[:, 0:CHUNK, :].rearrange("p j d -> p (j d)"),
+            in0=frac[:, 0:CHUNK, :].rearrange("p j d -> p (j d)"),
+            scalar=-1.0,
+            in1=frac[:, 0:CHUNK, :].rearrange("p j d -> p (j d)"),
+            op0=ALU.mult,
+            op1=ALU.max,
+        )
         nc.vector.tensor_copy(out=position[:, CHUNK:], in_=position_i[:, CHUNK:])
         make_cos_sin(0, CHUNK)
         gain = psum_acc.tile([P, 2, 2, 2, HALF], F32, name="acc")
@@ -171,8 +180,7 @@ def tile_gqaattention_pa_t_kernel(
         for hu in range(2):
             nc.tensor.matmul(out=gain[:, :, :, hu, :], lhsT=signs[:, 0, :], rhs=halves, start=True, stop=True)
         nc.tensor.matmul(out=gain[:, :, 0, 1, :], lhsT=signs[:, 1, :], rhs=halves[:, :, 0, :], start=True, stop=True)
-        for first_j in range(CHUNK, J, CHUNK):
-            make_angles(nc.vector, first_j, CHUNK)
+        make_angles(nc.vector, CHUNK, J - CHUNK)
         table = const.tile([P, J, 2, 2, 2, HALF], F32)
 
         def fold_gains(engine, first_j, count):
@@ -299,16 +307,20 @@ def tile_gqaattention_pa_t_kernel(
             nc.sync.dma_start(out=v_view[b, :, 0, slice(j, j + AT), :], in_=v_tiles[m][:])
         def ok(t): return 0 <= t < TILES
 
+        def load_behind(r):
+            c = r // CHUNK
+            if (r + 2) % CHUNK == 0 and c + X_BUFS < CHUNKS: load_chunk(c + X_BUFS)
         for g in range(-TRANSPOSE_AHEAD, PAIRS):
             p, r = 2 * (g + PROJECT_AHEAD), 2 * (g + TRANSPOSE_AHEAD)
             if ok(p):
                 project(p); project(p + 1)
                 squares(p); squares(p + 1); copy_v(p); copy_v(p + 1)
+
                 if (p // 2) % 2 == 0 or p == 2 * PAIRS - 2: root((p + 2) // 4)
+
             if ok(r):
                 transpose(r); transpose(r + 1); regroup(r); regroup(r + 1)
-                c = r // CHUNK
-                if (r + 2) % CHUNK == 0 and c + X_BUFS < CHUNKS: load_chunk(c + X_BUFS)
+                load_behind(r)
             if r == 0: make_cos_sin(CHUNK, CHUNK)
             if r == 2: make_cos_sin(2 * CHUNK, CHUNK)
             if r == 4:
@@ -316,6 +328,7 @@ def tile_gqaattention_pa_t_kernel(
                 nc.scalar.sqrt(out=warm[:, 1:2], in_=one[:])
             t = 2 * g
             if ok(t): rope(t); rope(t + 1)
+
             q = 2 * (g + QUANTISE_AHEAD)
             if g % 2 == 0 and (ok(t + 2) or ok(t + 4)):
                 n = (t + 4 + 2) // 4
@@ -326,5 +339,11 @@ def tile_gqaattention_pa_t_kernel(
             elif ok(q): quantise(q, 2)
             if g + TRANSPOSE_AHEAD < J // CHUNK: fold_gains(nc.vector, CHUNK * (g + TRANSPOSE_AHEAD), CHUNK)
             if ok(t):
-                add_terms(g, nc.gpsimd if g < PAIRS - 1 else nc.vector)
-                store_v(g); store(g)
+                if g < PAIRS - 1:
+                    add_terms(g)
+                    store(g)
+                else:
+                    for i in range(2):
+                        add_terms(g, nc.vector, i, 1)
+                        store(g, i, 1)
+            if ok(t + 2): store_v(g + 1)

@@ -36,7 +36,7 @@ QUANTISE_AHEAD = 4
 TRANSPOSE_AHEAD = 5
 ROUND_MAGIC = 1.5 * 2.0**23
 
-QT, NT, AT = 2, 4, 2
+QT, NT, AT = 2, 2, 2
 FLOPS = 2 * B * T * D * N_ALL
 
 
@@ -242,12 +242,12 @@ def tile_gqaattention_pa_t_kernel(
             acc_banks[t] = acc
 
         def squares(t):
-            n = (t + 2) // NT
-            if n not in sums_sq:
+            n = t // NT
+            if t % NT == 0:
                 sums_sq[n] = norm.tile([P, NT * ROPED], F32, name="sum_sq")
             junk = norm.tile([P, ROPED, HD], BF16, name="squares")
             for h in range(ROPED):
-                col = ROPED * ((t + 2) % NT) + h
+                col = ROPED * (t % NT) + h
                 nc.scalar.activation(out=junk[:, h, :], in_=acc_banks[t][:, HD * h : HD * (h + 1)], func=ACT.Square, accum_out=sums_sq[n][:, col : col + 1])
 
         def copy_v(t):
@@ -256,29 +256,27 @@ def tile_gqaattention_pa_t_kernel(
                 v_tiles[m] = results.tile([P, AT, HD], F32, name="v_sb")
             nc.scalar.copy(out=v_tiles[m][:, t % AT, :], in_=acc_banks[t][:, HD * ROPED :])
 
-        def span(n): return slice(2 * ROPED if n == 0 else 0, 2 * ROPED if n == TILES // 4 else 4 * ROPED)
-
         def root(n):
             lengths[n] = norm.tile([P, NT * ROPED], F32, name="length")
-            nc.scalar.sqrt(out=lengths[n][:, span(n)], in_=sums_sq[n][:, span(n)])
+            nc.scalar.sqrt(out=lengths[n][:], in_=sums_sq[n][:])
 
         def add_eps(n, engine=None):
             padded[n] = norm.tile([P, NT * ROPED], F32, name="padded")
-            if engine is None: nc.vector.tensor_scalar_add(out=padded[n][:, span(n)], in0=lengths[n][:, span(n)], scalar1=EPS)
-            else: nc.scalar.add(padded[n][:, span(n)], lengths[n][:, span(n)], EPS)
+            if engine is None: nc.vector.tensor_scalar_add(out=padded[n][:], in0=lengths[n][:], scalar1=EPS)
+            else: nc.scalar.add(padded[n][:], lengths[n][:], EPS)
 
         def invert(n):
             inverse[n] = norm.tile([P, NT * ROPED], F32, name="inverse")
-            nc.vector.reciprocal(out=inverse[n][:, span(n)], in_=padded[n][:, span(n)])
+            nc.vector.reciprocal(out=inverse[n][:], in_=padded[n][:])
 
         def rope(t):
             c, i, b, j = place(t)
-            m, n = t // AT, (t + 2) // NT
+            m, n = t // AT, t // NT
             if t % AT == 0:
                 term_tiles[m] = terms.tile([P, ROPED, AT, 2, 2, HALF], F32, name="terms")
             for h in range(ROPED):
                 which = 0 if h < Q_HEADS else 1
-                col = ROPED * ((t + 2) % NT) + h
+                col = ROPED * (t % NT) + h
                 nc.vector.scalar_tensor_tensor(
                     out=term_tiles[m][:, h, t % AT, :, :, :].rearrange("p r a d -> p r (a d)"),
                     in0=acc_banks[t][:, HD * h : HD * (h + 1)].unsqueeze(1).to_broadcast([P, 2, HD]),
@@ -316,7 +314,7 @@ def tile_gqaattention_pa_t_kernel(
                 project(p); project(p + 1)
                 squares(p); squares(p + 1); copy_v(p); copy_v(p + 1)
 
-                if (p // 2) % 2 == 0 or p == 2 * PAIRS - 2: root((p + 2) // 4)
+                root(p // 2)
 
             if ok(r):
                 transpose(r); transpose(r + 1); regroup(r); regroup(r + 1)
@@ -330,13 +328,10 @@ def tile_gqaattention_pa_t_kernel(
             if ok(t): rope(t); rope(t + 1)
 
             q = 2 * (g + QUANTISE_AHEAD)
-            if g % 2 == 0 and (ok(t + 2) or ok(t + 4)):
-                n = (t + 4 + 2) // 4
-                add_eps(n)
-                if ok(q): quantise(q, 1)
-                invert(n)
-                if ok(q): quantise(q + 1, 1)
-            elif ok(q): quantise(q, 2)
+            if ok(t + 2): add_eps(g + 1)
+            if ok(q): quantise(q, 1)
+            if ok(t + 2): invert(g + 1)
+            if ok(q): quantise(q + 1, 1)
             if g + TRANSPOSE_AHEAD < J // CHUNK: fold_gains(nc.vector, CHUNK * (g + TRANSPOSE_AHEAD), CHUNK)
             if ok(t):
                 if g < PAIRS - 1:

@@ -317,7 +317,9 @@ def tile_gqaattention_pa_t_kernel(
                 root(p // 2)
 
             if ok(r):
-                transpose(r); transpose(r + 1); regroup(r); regroup(r + 1)
+                transpose(r); transpose(r + 1); regroup(r)
+                if ok(p): add_eps(p // 2, nc.scalar)
+                regroup(r + 1)
                 load_behind(r)
             if r == 0: make_cos_sin(CHUNK, CHUNK)
             if r == 2: make_cos_sin(2 * CHUNK, CHUNK)
@@ -328,7 +330,7 @@ def tile_gqaattention_pa_t_kernel(
             if ok(t): rope(t); rope(t + 1)
 
             q = 2 * (g + QUANTISE_AHEAD)
-            if ok(t + 2): add_eps(g + 1)
+            if not ok(r) and ok(p): add_eps(p // 2, nc.scalar)
             if ok(q): quantise(q, 1)
             if ok(t + 2): invert(g + 1)
             if ok(q): quantise(q + 1, 1)

@@ -136,7 +136,7 @@ def tile_gqaattention_pa_t_kernel(
                 )
             width *= 4
             if width == 4:
-                nc.vector.tensor_copy(out=position[:, 0:CHUNK], in_=position_i[:, 0:CHUNK])
+                nc.vector.tensor_copy(out=position[:], in_=position_i[:])
             if width == 16:
                 nc.vector.tensor_scalar_mul(out=quarter_turn[:], in0=one[:], scalar1=math.pi / 2)
         load_chunk(1)
@@ -153,7 +153,7 @@ def tile_gqaattention_pa_t_kernel(
         def make_angles(engine, first_j, count):
             js = slice(first_j, first_j + count)
             shape = [P, count, HALF]
-            engine.tensor_tensor(out=frac[:, js, :], in0=position[:, js].unsqueeze(2).to_broadcast(shape), in1=per_position[:].unsqueeze(1).to_broadcast(shape), op=ALU.mult)
+            if first_j == 0: engine.tensor_tensor(out=frac[:, js, :], in0=position[:, js].unsqueeze(2).to_broadcast(shape), in1=per_position[:].unsqueeze(1).to_broadcast(shape), op=ALU.mult)
             engine.tensor_scalar(out=whole[:, js, :], in0=frac[:, js, 0:WRAP], scalar1=ROUND_MAGIC, scalar2=ROUND_MAGIC, op0=ALU.add, op1=ALU.subtract)
             engine.tensor_tensor(out=frac[:, js, 0:WRAP], in0=frac[:, js, 0:WRAP], in1=whole[:, js, :], op=ALU.subtract)
 
@@ -164,6 +164,8 @@ def tile_gqaattention_pa_t_kernel(
             nc.scalar.activation(out=cos_sin[:, js, 1, :], in_=frac[:, js, :], func=ACT.Sin, scale=2.0 * math.pi)
             nc.scalar.activation(out=cos_sin[:, js, 0, :], in_=absolute[:, js, :], func=ACT.Sin, scale=-2.0 * math.pi, bias=quarter_turn[:])
 
+        for j in range(CHUNK, J):
+            nc.scalar.activation(out=frac[:, j, :], in_=per_position[:], func=ACT.Copy, scale=position[:, j : j + 1])
         make_angles(nc.vector, 0, CHUNK)
         nc.vector.scalar_tensor_tensor(
             out=absolute[:, 0:CHUNK, :].rearrange("p j d -> p (j d)"),
@@ -173,7 +175,6 @@ def tile_gqaattention_pa_t_kernel(
             op0=ALU.mult,
             op1=ALU.max,
         )
-        nc.vector.tensor_copy(out=position[:, CHUNK:], in_=position_i[:, CHUNK:])
         make_cos_sin(0, CHUNK)
         gain = psum_acc.tile([P, 2, 2, 2, HALF], F32, name="acc")
         halves = gamma_rows[:].rearrange("p a (h d) -> p a h d", h=2)
@@ -250,11 +251,15 @@ def tile_gqaattention_pa_t_kernel(
                 col = ROPED * (t % NT) + h
                 nc.scalar.activation(out=junk[:, h, :], in_=acc_banks[t][:, HD * h : HD * (h + 1)], func=ACT.Square, accum_out=sums_sq[n][:, col : col + 1])
 
+        def on_vector(t):
+            return t % 8 == 7 and t < TILES - 8
+
         def copy_v(t):
             m = t // AT
             if t % AT == 0:
                 v_tiles[m] = results.tile([P, AT, HD], F32, name="v_sb")
-            nc.scalar.copy(out=v_tiles[m][:, t % AT, :], in_=acc_banks[t][:, HD * ROPED :])
+            if not on_vector(t):
+                nc.scalar.copy(out=v_tiles[m][:, t % AT, :], in_=acc_banks[t][:, HD * ROPED :])
 
         def root(n):
             lengths[n] = norm.tile([P, NT * ROPED], F32, name="length")
@@ -327,13 +332,18 @@ def tile_gqaattention_pa_t_kernel(
                 make_cos_sin(3 * CHUNK, CHUNK)
                 nc.scalar.sqrt(out=warm[:, 1:2], in_=one[:])
             t = 2 * g
-            if ok(t): rope(t); rope(t + 1)
+            if ok(t): rope(t)
+            if ok(t + 2) and not ok(t + 8): invert(g + 1)
+            if ok(t): rope(t + 1)
+            if ok(t) and on_vector(t + 1):
+                nc.vector.tensor_copy(out=v_tiles[g][:, 1, :], in_=acc_banks[t + 1][:, HD * ROPED :])
+                store_v(g)
 
             q = 2 * (g + QUANTISE_AHEAD)
             if not ok(r) and ok(p): add_eps(p // 2, nc.scalar)
-            if ok(q): quantise(q, 1)
-            if ok(t + 2): invert(g + 1)
-            if ok(q): quantise(q + 1, 1)
+            if ok(t + 2) and ok(q): invert(g + 1)
+            if ok(q): quantise(q, 2)
+            if ok(p) and not on_vector(p + 1): store_v(g + PROJECT_AHEAD)
             if g + TRANSPOSE_AHEAD < J // CHUNK: fold_gains(nc.vector, CHUNK * (g + TRANSPOSE_AHEAD), CHUNK)
             if ok(t):
                 if g < PAIRS - 1:
@@ -343,4 +353,3 @@ def tile_gqaattention_pa_t_kernel(
                     for i in range(2):
                         add_terms(g, nc.vector, i, 1)
                         store(g, i, 1)
-            if ok(t + 2): store_v(g + 1)

import math
from contextlib import ExitStack

import concourse.mybir as mybir
from concourse.masks import make_identity

F32 = mybir.dt.float32
BF16 = mybir.dt.bfloat16
I32 = mybir.dt.int32
U32 = mybir.dt.uint32
U8 = mybir.dt.uint8
FP8X4 = mybir.dt.float8_e4m3fn_x4
ALU = mybir.AluOpType
ACT = mybir.ActivationFunctionType

P = 128
B, T, D = 4, 2048, 1024
HD = 128
HALF = HD // 2
Q_HEADS = 2
ROPED = Q_HEADS + 1
N_ALL = (ROPED + 1) * HD
K_PASS = 4 * P
PASSES = D // K_PASS
ROPE_BASE = 10000.0
EPS = 1e-6

J = T // P
CHUNK = 4
PAIR = 2
CHUNKS = B * J // CHUNK
PAIRS = CHUNKS * CHUNK // PAIR
X_BUFS = 4
PROJECT_AHEAD = 2
QUANTISE_AHEAD = 4
TRANSPOSE_AHEAD = 5
ROUND_MAGIC = 1.5 * 2.0**23

QT, NT, AT = 2, 2, 2
FLOPS = 2 * B * T * D * N_ALL


def tile_gqaattention_pa_t_kernel(
    tc,
    x,
    wq_words,
    wq_scales,
    wk_words,
    wk_scales,
    wv_words,
    wv_scales,
    gamma_q,
    gamma_k,
    out_0,
    out_1,
    out_2,
):
    nc = tc.nc
    with ExitStack() as ctx:
        ctx.enter_context(tc.manual_schedule())
        const = ctx.enter_context(tc.tile_pool(name="const", bufs=1))
        x_pool = ctx.enter_context(tc.tile_pool(name="x", bufs=X_BUFS))
        quant = ctx.enter_context(tc.tile_pool(name="quant", bufs=5))
        norm = ctx.enter_context(tc.tile_pool(name="norm", bufs=6))
        terms = ctx.enter_context(tc.tile_pool(name="terms", bufs=5))
        results = ctx.enter_context(tc.tile_pool(name="results", bufs=8))
        psum_xt = ctx.enter_context(tc.psum_pool(name="psum_xt", bufs=PAIR))
        psum_acc = ctx.enter_context(tc.psum_pool(name="psum_acc", bufs=(PROJECT_AHEAD + 1) * PAIR))

        x_view = x.rearrange("b (p j) k -> b p j k", j=J)
        q_view = out_0.rearrange("b h (p j) d -> b p h j d", j=J)
        k_view = out_1.rearrange("b h (p j) d -> b p h j d", j=J)
        v_view = out_2.rearrange("b h (p j) d -> b p h j d", j=J)

        x_tiles = {}

        def load_chunk(c):
            j0, b = CHUNK * (c // B), c % B
            x_sb = x_pool.tile([P, CHUNK, D], BF16, name="x_sb")
            pieces = 4 if c == 0 else 1
            width = CHUNK // pieces
            for first_tile in range(0, CHUNK, width):
                nc.sync.dma_start(
                    out=x_sb[:, first_tile : first_tile + width, :],
                    in_=x_view[b, :, j0 + first_tile : j0 + first_tile + width, :],
                )
            x_tiles[c] = x_sb


        gamma_rows = const.tile([P, 2, HD], BF16)
        signs = const.tile([P, 2, P], BF16)
        one = const.tile([P, 1], F32)
        nc.vector.memset(gamma_rows[:], 0.0)
        nc.vector.memset(one[:], 1.0)
        warm = const.tile([P, 2], F32)
        nc.scalar.activation(out=warm[:, 0:1], in_=one[:], func=ACT.Sin)
        position_i = const.tile([P, J], I32)
        nc.gpsimd.iota(position_i[:], pattern=[[1, J]], base=0, channel_multiplier=J)
        ident = const.tile([P, P], F32)
        make_identity(nc, ident[:])
        w_words = const.tile([P, PASSES, N_ALL], U32, align_bytes=64)
        w_scales = const.tile([P, PASSES, N_ALL], U8, align_bytes=64)
        nc.sync.dma_start(out=gamma_rows[0:1, 0, :], in_=gamma_q.unsqueeze(0))
        nc.sync.dma_start(out=gamma_rows[0:1, 1, :], in_=gamma_k.unsqueeze(0))
        load_chunk(0)
        groups = ((wq_words, wq_scales), (wk_words, wk_scales), (wv_words, wv_scales))
        def load_words():
            first = 0
            for words, scales in groups:
                cols = slice(first, first + words.shape[2])
                first += words.shape[2]
                nc.sync.dma_start(out=w_words[:, :, cols].bitcast(I32), in_=words.rearrange("g p n t -> p g (n t)").bitcast(I32))
        def load_scales():
            first = 0
            for words, scales in groups:
                cols = slice(first, first + words.shape[2])
                first += words.shape[2]
                for quadrant in range(4):
                    nc.sync.dma_start(
                        out=w_scales[32 * quadrant : 32 * quadrant + 4, :, cols].bitcast(I32),
                        in_=scales[:, 4 * quadrant : 4 * quadrant + 4, :].rearrange("g r n -> r g n").bitcast(I32))
        quarter_turn = const.tile([P, 1], F32)
        position = const.tile([P, J], F32)
        per_position = const.tile([P, HALF], F32)
        nc.vector.tensor_scalar_mul(out=per_position[:, 0:1], in0=one[:], scalar1=1.0 / (2.0 * math.pi))
        nc.vector.memset(signs[:, 0, :], 1.0)
        nc.vector.memset(signs[:, 1, :], -1.0)
        nc.vector.memset(w_scales[:].bitcast(I32), 0)
        width = 1
        while width < HALF:
            for copy in range(1, 4):
                nc.vector.tensor_scalar_mul(
                    out=per_position[:, copy * width : (copy + 1) * width],
                    in0=per_position[:, 0:width],
                    scalar1=ROPE_BASE ** (-copy * width / HALF),
                )
            width *= 4
            if width == 4:
                nc.vector.tensor_copy(out=position[:], in_=position_i[:])
            if width == 16:
                nc.vector.tensor_scalar_mul(out=quarter_turn[:], in0=one[:], scalar1=math.pi / 2)
        load_chunk(1)
        load_words()
        load_scales()
        for c in range(2, X_BUFS):
            load_chunk(c)
        WRAP = sum(1 for d in range(HALF) if (T - 1) * ROPE_BASE ** (-d / HALF) > math.pi)
        whole = const.tile([P, J, WRAP], F32)
        frac = const.tile([P, J, HALF], F32)
        absolute = const.tile([P, J, HALF], F32)
        cos_sin = const.tile([P, J, 2, HALF], F32)

        def make_angles(engine, first_j, count):
            js = slice(first_j, first_j + count)
            shape = [P, count, HALF]
            if first_j == 0: engine.tensor_tensor(out=frac[:, js, :], in0=position[:, js].unsqueeze(2).to_broadcast(shape), in1=per_position[:].unsqueeze(1).to_broadcast(shape), op=ALU.mult)
            engine.tensor_scalar(out=whole[:, js, :], in0=frac[:, js, 0:WRAP], scalar1=ROUND_MAGIC, scalar2=ROUND_MAGIC, op0=ALU.add, op1=ALU.subtract)
            engine.tensor_tensor(out=frac[:, js, 0:WRAP], in0=frac[:, js, 0:WRAP], in1=whole[:, js, :], op=ALU.subtract)

        def make_cos_sin(first_j, count):
            js = slice(first_j, first_j + count)
            if first_j:
                nc.scalar.activation(out=absolute[:, js, :], in_=frac[:, js, :], func=ACT.Abs)
            nc.scalar.activation(out=cos_sin[:, js, 1, :], in_=frac[:, js, :], func=ACT.Sin, scale=2.0 * math.pi)
            nc.scalar.activation(out=cos_sin[:, js, 0, :], in_=absolute[:, js, :], func=ACT.Sin, scale=-2.0 * math.pi, bias=quarter_turn[:])

        for j in range(CHUNK, J):
            nc.scalar.activation(out=frac[:, j, :], in_=per_position[:], func=ACT.Copy, scale=position[:, j : j + 1])
        make_angles(nc.vector, 0, CHUNK)
        nc.vector.scalar_tensor_tensor(
            out=absolute[:, 0:CHUNK, :].rearrange("p j d -> p (j d)"),
            in0=frac[:, 0:CHUNK, :].rearrange("p j d -> p (j d)"),
            scalar=-1.0,
            in1=frac[:, 0:CHUNK, :].rearrange("p j d -> p (j d)"),
            op0=ALU.mult,
            op1=ALU.max,
        )
        make_cos_sin(0, CHUNK)
        gain = psum_acc.tile([P, 2, 2, 2, HALF], F32, name="acc")
        halves = gamma_rows[:].rearrange("p a (h d) -> p a h d", h=2)
        for hu in range(2):
            nc.tensor.matmul(out=gain[:, :, :, hu, :], lhsT=signs[:, 0, :], rhs=halves, start=True, stop=True)
        nc.tensor.matmul(out=gain[:, :, 0, 1, :], lhsT=signs[:, 1, :], rhs=halves[:, :, 0, :], start=True, stop=True)
        make_angles(nc.vector, CHUNK, J - CHUNK)
        table = const.tile([P, J, 2, 2, 2, HALF], F32)

        def fold_gains(engine, first_j, count):
            js = slice(first_j, first_j + count)
            shape = [P, count, 2, HD]
            engine.tensor_tensor(
                out=table[:, js, :, 0, :, :].rearrange("p j a h d -> p j a (h d)"),
                in0=cos_sin[:, js].rearrange("p j r d -> p j (r d)").unsqueeze(2).to_broadcast(shape),
                in1=gain[:, :, 0, :, :].rearrange("p a h d -> p a (h d)").unsqueeze(1).to_broadcast(shape), op=ALU.mult)
            shape = [P, count, 2, HALF]
            for half in range(2):
                engine.tensor_tensor(
                    out=table[:, js, :, 1, half, :],
                    in0=cos_sin[:, js, 1 - half, :].unsqueeze(2).to_broadcast(shape),
                    in1=gain[:, :, 1, half, :].unsqueeze(1).to_broadcast(shape), op=ALU.mult)

        xt_banks, x_codes, x_scales, grouped_tiles = {}, {}, {}, {}
        acc_banks, sums_sq, lengths, padded, inverse = {}, {}, {}, {}, {}
        v_tiles, out_tiles, term_tiles = {}, {}, {}
        TILES = B * J

        def place(t):
            c = t // CHUNK
            return c, t % CHUNK, c % B, CHUNK * (c // B) + t % CHUNK

        def transpose(t):
            c, i, b, j = place(t)
            words = x_tiles[c][:].bitcast(F32).rearrange("p j (s w u) -> p j s u w", s=PASSES, u=2)
            xt = psum_xt.tile([P, PASSES, 2, P], F32, name="xt")
            for s in range(PASSES):
                for u in range(2):
                    nc.tensor.transpose(xt[:, s, u, :], words[:, i, s, u, :], ident[:])
            xt_banks[t] = xt

        def regroup(t):
            q = t // QT
            if t % QT == 0:
                grouped_tiles[q] = quant.tile([P, QT, PASSES, P, 4], BF16, name="grouped", align_bytes=64)
                x_codes[q] = quant.tile([P, QT, PASSES, P], U32, name="codes", align_bytes=64)
                x_scales[q] = quant.tile([P, QT, PASSES, P], U8, name="scales", align_bytes=64)
            nc.scalar.copy(out=grouped_tiles[q][:, t % QT].bitcast(F32), in_=xt_banks[t][:].rearrange("p s u t -> p s t u"))

        def quantise(t, count):
            q = t // QT
            tiles = slice(t % QT, t % QT + count)
            nc.vector.quantize_mx(
                out=x_codes[q][:, tiles].rearrange("p i s t -> p (i s t)").bitcast(FP8X4),
                scales=x_scales[q][:, tiles].rearrange("p i s t -> p (i s t)"),
                in_=grouped_tiles[q][:, tiles].rearrange("p i s t e -> p (i s t e)"),
            )

        def project(t):
            q, i = t // QT, t % QT
            acc = psum_acc.tile([P, N_ALL], F32, name="acc")
            for s in range(PASSES):
                nc.tensor.matmul_mx(
                    out=acc[:], lhsT=x_codes[q][:, i, s, :].bitcast(FP8X4), lhsT_scale=x_scales[q][:, i, s, :],
                    rhs=w_words[:, s, :].bitcast(FP8X4), rhs_scale=w_scales[:, s, :], start=(s == 0), stop=(s == PASSES - 1))
            acc_banks[t] = acc

        def squares(t):
            n = t // NT
            if t % NT == 0:
                sums_sq[n] = norm.tile([P, NT * ROPED], F32, name="sum_sq")
            junk = norm.tile([P, ROPED, HD], BF16, name="squares")
            for h in range(ROPED):
                col = ROPED * (t % NT) + h
                nc.scalar.activation(out=junk[:, h, :], in_=acc_banks[t][:, HD * h : HD * (h + 1)], func=ACT.Square, accum_out=sums_sq[n][:, col : col + 1])

        def on_vector(t):
            return t % 8 == 7 and t < TILES - 8

        def copy_v(t):
            m = t // AT
            if t % AT == 0:
                v_tiles[m] = results.tile([P, AT, HD], F32, name="v_sb")
            if not on_vector(t):
                nc.scalar.copy(out=v_tiles[m][:, t % AT, :], in_=acc_banks[t][:, HD * ROPED :])

        def root(n):
            lengths[n] = norm.tile([P, NT * ROPED], F32, name="length")
            nc.scalar.sqrt(out=lengths[n][:], in_=sums_sq[n][:])

        def add_eps(n, engine=None):
            padded[n] = norm.tile([P, NT * ROPED], F32, name="padded")
            if engine is None: nc.vector.tensor_scalar_add(out=padded[n][:], in0=lengths[n][:], scalar1=EPS)
            else: nc.scalar.add(padded[n][:], lengths[n][:], EPS)

        def invert(n):
            inverse[n] = norm.tile([P, NT * ROPED], F32, name="inverse")
            nc.vector.reciprocal(out=inverse[n][:], in_=padded[n][:])

        def rope(t):
            c, i, b, j = place(t)
            m, n = t // AT, t // NT
            if t % AT == 0:
                term_tiles[m] = terms.tile([P, ROPED, AT, 2, 2, HALF], F32, name="terms")
            for h in range(ROPED):
                which = 0 if h < Q_HEADS else 1
                col = ROPED * (t % NT) + h
                nc.vector.scalar_tensor_tensor(
                    out=term_tiles[m][:, h, t % AT, :, :, :].rearrange("p r a d -> p r (a d)"),
                    in0=acc_banks[t][:, HD * h : HD * (h + 1)].unsqueeze(1).to_broadcast([P, 2, HD]),
                    scalar=inverse[n][:, col : col + 1],
                    in1=table[:, j, which, :, :, :].rearrange("p r a d -> p r (a d)"),
                    op0=ALU.mult, op1=ALU.mult)

        def add_terms(m, engine=None, first=0, count=None):
            count = count or AT
            if first == 0:
                out_tiles[m] = results.tile([P, ROPED, AT, 2, HALF], F32, name="qk_sb")
            sl = slice(first, first + count)
            (engine or nc.gpsimd).tensor_tensor(out=out_tiles[m][:, :, sl], in0=term_tiles[m][:, :, sl, :, 0, :], in1=term_tiles[m][:, :, sl, :, 1, :], op=ALU.add)

        def store(m, first=0, count=None):
            count = count or AT
            c, i, b, j = place(m * AT + first)
            js = slice(j, j + count)
            sl = slice(first, first + count)
            qk = out_tiles[m][:].rearrange("p h i a d -> p h i (a d)")
            nc.sync.dma_start(out=q_view[b, :, :, js, :], in_=qk[:, 0:Q_HEADS, sl, :])
            nc.sync.dma_start(out=k_view[b, :, 0, js, :], in_=qk[:, Q_HEADS, sl, :])

        def store_v(m):
            c, i, b, j = place(m * AT)
            nc.sync.dma_start(out=v_view[b, :, 0, slice(j, j + AT), :], in_=v_tiles[m][:])
        def ok(t): return 0 <= t < TILES

        def load_behind(r):
            c = r // CHUNK
            if (r + 2) % CHUNK == 0 and c + X_BUFS < CHUNKS: load_chunk(c + X_BUFS)
        for g in range(-TRANSPOSE_AHEAD, PAIRS):
            p, r = 2 * (g + PROJECT_AHEAD), 2 * (g + TRANSPOSE_AHEAD)
            if ok(p):
                project(p); project(p + 1)
                squares(p); squares(p + 1); copy_v(p); copy_v(p + 1)

                root(p // 2)

            if ok(r):
                transpose(r); transpose(r + 1); regroup(r)
                if ok(p): add_eps(p // 2, nc.scalar)
                regroup(r + 1)
                load_behind(r)
            if r == 0: make_cos_sin(CHUNK, CHUNK)
            if r == 2: make_cos_sin(2 * CHUNK, CHUNK)
            if r == 4:
                make_cos_sin(3 * CHUNK, CHUNK)
                nc.scalar.sqrt(out=warm[:, 1:2], in_=one[:])
            t = 2 * g
            if ok(t): rope(t)
            if ok(t + 2) and not ok(t + 8): invert(g + 1)
            if ok(t): rope(t + 1)
            if ok(t) and on_vector(t + 1):
                nc.vector.tensor_copy(out=v_tiles[g][:, 1, :], in_=acc_banks[t + 1][:, HD * ROPED :])
                store_v(g)

            q = 2 * (g + QUANTISE_AHEAD)
            if not ok(r) and ok(p): add_eps(p // 2, nc.scalar)
            if ok(t + 2) and ok(q): invert(g + 1)
            if ok(q): quantise(q, 2)
            if ok(p) and not on_vector(p + 1): store_v(g + PROJECT_AHEAD)
            if g + TRANSPOSE_AHEAD < J // CHUNK: fold_gains(nc.vector, CHUNK * (g + TRANSPOSE_AHEAD), CHUNK)
            if ok(t):
                if g < PAIRS - 1:
                    add_terms(g)
                    store(g)
                else:
                    for i in range(2):
                        add_terms(g, nc.vector, i, 1)
                        store(g, i, 1)
